import numpy as np
import ml_dtypes


def mxq(x, axis, fmt="e4m3"):
    dtype, down = {"e4m3": (ml_dtypes.float8_e4m3fn, 7), "e5m2": (ml_dtypes.float8_e5m2, 14)}[fmt]
    v = np.moveaxis(np.asarray(x, np.float32).astype(ml_dtypes.bfloat16).astype(np.float64), axis, -1)
    blocks = v.reshape(v.shape[:-1] + (-1, 32))
    amax = np.abs(blocks).max(-1, keepdims=True)
    byte = np.maximum(np.where(amax > 0, np.frexp(amax)[1] - 1 + 127, 0) - down, 1)
    scale = np.exp2(byte - 127.0)
    codes = (blocks / scale).astype(np.float32).astype(dtype).astype(np.float64)
    return np.moveaxis((codes * scale).reshape(v.shape), -1, axis)


WIDE = False


def mx_kscale(k):
    if not WIDE:
        return np.ones(k)
    levels = np.array([10, -10, 5, -5, 0])
    a = np.random.permutation(np.resize(levels, k // 512 * 4)).reshape(k // 512, 4)
    idx = np.arange(k)
    return np.exp2(a[idx // 512, idx % 128 // 32])


BF16 = ml_dtypes.bfloat16


def bf(x):
    return np.asarray(x, np.float32).astype(BF16)


def f64(x):
    return np.asarray(x).astype(np.float64)


NU, NI, D = 8192, 512, 512
EPS_NORM = 1e-8
CLAMP_MIN = 1e-6
CLAMP_MAX = 1.0


def setup_inputs():
    s = mx_kscale(D)
    return {"h_user": bf(np.maximum(np.random.standard_normal((NU, D)), 0.0) * 0.8 * s),
            "h_item": bf(np.maximum(np.random.standard_normal((NI, D)), 0.0) * 0.8 * s),
            "uW2": bf(np.random.standard_normal((D, D)) / np.sqrt(D) / s[:, None]),
            "ub2": bf(np.random.standard_normal(D) * 0.1),
            "iW2": bf(np.random.standard_normal((D, D)) / np.sqrt(D) / s[:, None]),
            "ib2": bf(np.random.standard_normal(D) * 0.1)}


def reference(h_user, h_item, uW2, ub2, iW2, ib2):
    u = (mxq(f64(h_user), 1, "e4m3") @ mxq(f64(uW2), 0, "e4m3")) + f64(ub2)
    it = (mxq(f64(h_item), 1, "e4m3") @ mxq(f64(iW2), 0, "e4m3")) + f64(ib2)
    un = u / np.maximum(np.sqrt((u * u).sum(1, keepdims=True)), EPS_NORM)
    itn = it / np.maximum(np.sqrt((it * it).sum(1, keepdims=True)), EPS_NORM)
    sim = mxq(un, 1, "e4m3") @ mxq(itn, 1, "e4m3").T
    return np.clip(sim, CLAMP_MIN, CLAMP_MAX)

@@ -1,0 +1,215 @@
+from contextlib import ExitStack
+
+import concourse.mybir as mybir
+from concourse.masks import make_identity
+
+F32 = mybir.dt.float32
+BF16 = mybir.dt.bfloat16
+U32 = mybir.dt.uint32
+U8 = mybir.dt.uint8
+FP8X4 = mybir.dt.float8_e4m3fn_x4
+ALU = mybir.AluOpType
+ACTF = mybir.ActivationFunctionType
+
+P = 128
+D = 512
+NU = 8192
+NI = 512
+GROUP = 8
+HALF = 4
+EPS_NORM = 1e-8
+CLAMP_MIN = 1e-6
+CLAMP_MAX = 1.0
+
+FLOPS = 2 * NU * D * D + 2 * NI * D * D + 2 * NU * D * NI
+
+
+def tile_net_pb_t_kernel(tc, h_user, h_item, uW2, ub2, iW2, ib2, out):
+    nc = tc.nc
+    with ExitStack() as ctx:
+        const = ctx.enter_context(tc.tile_pool(name="const", bufs=1))
+        xpool = ctx.enter_context(tc.tile_pool(name="xpool", bufs=1))
+        stage = ctx.enter_context(tc.tile_pool(name="stage", bufs=3))
+        vpool = ctx.enter_context(tc.tile_pool(name="vpool", bufs=6))
+        small = ctx.enter_context(tc.tile_pool(name="small", bufs=4))
+        opool = ctx.enter_context(tc.tile_pool(name="opool", bufs=4))
+        ps_h = ctx.enter_context(tc.psum_pool(name="ps_h", bufs=2))
+        ps_u = ctx.enter_context(tc.psum_pool(name="ps_u", bufs=2))
+        ps_t = ctx.enter_context(tc.psum_pool(name="ps_t", bufs=2))
+        ps_s = ctx.enter_context(tc.psum_pool(name="ps_s", bufs=2))
+
+        one = const.tile([P, 1], F32, name="one")
+        nc.vector.memset(one[:], 1.0)
+        warm = const.tile([P, 1], F32, name="warm")
+        nc.scalar.activation(out=warm[:], in_=one[:], func=ACTF.Sqrt)
+
+        ident_f = const.tile([P, P], F32, name="ident_f")
+        make_identity(nc, ident_f[:])
+        ident_b = const.tile([P, P], BF16, name="ident_b")
+        make_identity(nc, ident_b[:])
+
+        xi = xpool.tile([P, NI // P, D], BF16, name="xi")
+        nc.sync.dma_start(out=xi[:], in_=h_item.rearrange("(j p) k -> p j k", p=P))
+
+        def load_weight(w, b, nm):
+            raw = const.tile([P, 4, D], BF16, name="raw_" + nm)
+            nc.sync.dma_start(
+                out=raw[:].rearrange("q (u e) c -> q u e c", u=2),
+                in_=w.rearrange("(u q e) c -> q u e c", u=2, e=2),
+            )
+            bb = const.tile([P, D], BF16, name="bias_" + nm)
+            nc.sync.dma_start(out=bb[:], in_=b.partition_broadcast(P))
+            return raw, bb
+
+        raw_i, bias_i = load_weight(iW2, ib2, "i")
+        n_groups = NU // (P * GROUP)
+        xs = []
+        for g in range(n_groups):
+            xg = xpool.tile([P, GROUP, D], BF16, name="x%d" % g)
+            xs.append(xg)
+        rows = P * GROUP
+        nc.sync.dma_start(out=xs[0][:], in_=h_user[0:rows, :].rearrange("(p j) k -> p j k", j=GROUP))
+        raw_u, bias_u = load_weight(uW2, ub2, "u")
+        for g in range(1, n_groups):
+            nc.sync.dma_start(
+                out=xs[g][:],
+                in_=h_user[g * rows : (g + 1) * rows, :].rearrange("(p j) k -> p j k", j=GROUP),
+            )
+
+        def quantise_weight(raw, nm):
+            grouped = const.tile([P, D, 4], BF16, name="wg_" + nm, align_bytes=64)
+            nc.vector.tensor_copy(out=grouped[:], in_=raw[:].rearrange("p t c -> p c t"))
+            codes = const.tile([P, D], U32, name="wc_" + nm, align_bytes=64)
+            scales = const.tile([P, D], U8, name="ws_" + nm, align_bytes=64)
+            nc.vector.quantize_mx(
+                out=codes[:].bitcast(FP8X4),
+                scales=scales[:],
+                in_=grouped[:].rearrange("p c t -> p (c t)"),
+            )
+            return codes, scales
+
+        wc_i, ws_i = quantise_weight(raw_i, "i")
+        wc_u, ws_u = quantise_weight(raw_u, "u")
+
+        itc = const.tile([P, NI], U32, name="itc", align_bytes=64)
+        its = const.tile([P, NI], U8, name="its", align_bytes=64)
+
+        out_v = out.rearrange("(g p h j) n -> g h p j n", p=P, h=GROUP // HALF, j=HALF)
+
+        pairs = []
+        for k in range(NI // (2 * P)):
+            pairs.append({"x": xi, "j0": 2 * k, "wc": wc_i, "ws": ws_i, "bias": bias_i, "item": k})
+        for g in range(n_groups):
+            for k in range(GROUP // 2):
+                pairs.append({"x": xs[g], "j0": 2 * k, "wc": wc_u, "ws": ws_u, "bias": bias_u, "item": None, "g": g})
+        o_tiles = {}
+
+        def stage_a(pr):
+            hT = ps_h.tile([P, 2, 2, P], F32, name="hT")
+            for j in range(2):
+                xw = pr["x"][:, pr["j0"] + j, :].bitcast(F32)
+                for u in range(2):
+                    nc.tensor.transpose(hT[:, j, u, :], xw[:, u * P : (u + 1) * P], ident_f[:])
+            hg = stage.tile([P, 2 * D], BF16, name="hg", align_bytes=64)
+            nc.scalar.copy(
+                out=hg[:].bitcast(F32).rearrange("p (j r u) -> p j r u", j=2, u=2),
+                in_=hT[:].rearrange("p j u r -> p j r u"),
+            )
+            pr["hg"] = hg
+
+        def stage_b(pr):
+            hc = stage.tile([P, 2 * P], U32, name="hc", align_bytes=64)
+            hs = stage.tile([P, 2 * P], U8, name="hs", align_bytes=64)
+            nc.vector.quantize_mx(out=hc[:].bitcast(FP8X4), scales=hs[:], in_=pr["hg"][:])
+            ss = small.tile([P, 2], F32, name="ss")
+            pr["v"] = []
+            for j in range(2):
+                cols = slice(j * P, (j + 1) * P)
+                u_ps = ps_u.tile([P, D], F32, name="u_ps")
+                nc.tensor.matmul_mx(
+                    out=u_ps[:],
+                    lhsT=hc[:, cols].bitcast(FP8X4),
+                    lhsT_scale=hs[:, cols],
+                    rhs=pr["wc"][:].bitcast(FP8X4),
+                    rhs_scale=pr["ws"][:],
+                    start=True,
+                    stop=True,
+                )
+                v = vpool.tile([P, D], F32, name="v")
+                nc.vector.tensor_tensor(out=v[:], in0=u_ps[:], in1=pr["bias"][:], op=ALU.add)
+                junk = stage.tile([P, D], BF16, name="junk")
+                nc.scalar.activation(out=junk[:], in_=v[:], func=ACTF.Square, accum_out=ss[:, j : j + 1])
+                pr["v"].append(v)
+            nrm = small.tile([P, 2], F32, name="nrm")
+            nc.scalar.activation(out=nrm[:], in_=ss[:], func=ACTF.Sqrt)
+            nrc = small.tile([P, 2], F32, name="nrc")
+            nc.vector.tensor_scalar_max(out=nrc[:], in0=nrm[:], scalar1=EPS_NORM)
+            rn = small.tile([P, 2], F32, name="rn")
+            nc.vector.reciprocal(out=rn[:], in_=nrc[:])
+            pr["rn"] = rn
+
+        def stage_c(pr):
+            unT = ps_t.tile([P, 2, 4, P], BF16, name="unT")
+            for j in range(2):
+                un = vpool.tile([P, D], BF16, name="un")
+                nc.gpsimd.tensor_scalar(
+                    out=un[:],
+                    in0=pr["v"][j][:],
+                    scalar1=pr["rn"][:, j : j + 1],
+                    scalar2=0.0,
+                    op0=ALU.mult,
+                    op1=ALU.add,
+                )
+                for t in range(4):
+                    nc.tensor.transpose(unT[:, j, t, :], un[:, t * P : (t + 1) * P], ident_b[:])
+            ug = stage.tile([P, 2 * D], BF16, name="ug", align_bytes=64)
+            nc.scalar.copy(
+                out=ug[:].rearrange("p (j r t) -> p j r t", j=2, t=4),
+                in_=unT[:].rearrange("p j t r -> p j r t"),
+            )
+            pr["ug"] = ug
+
+        def stage_d(pr):
+            if pr["item"] is not None:
+                cols = slice(pr["item"] * 2 * P, (pr["item"] + 1) * 2 * P)
+                nc.vector.quantize_mx(out=itc[:, cols].bitcast(FP8X4), scales=its[:, cols], in_=pr["ug"][:])
+                return
+            uc = stage.tile([P, 2 * P], U32, name="uc", align_bytes=64)
+            us = stage.tile([P, 2 * P], U8, name="us", align_bytes=64)
+            nc.vector.quantize_mx(out=uc[:].bitcast(FP8X4), scales=us[:], in_=pr["ug"][:])
+            g = pr["g"]
+            hh = pr["j0"] // HALF
+            if pr["j0"] % HALF == 0:
+                o_new = opool.tile([P, HALF, NI], F32, name="o")
+                o_tiles[(g, hh)] = o_new
+            o = o_tiles[(g, hh)]
+            for j in range(2):
+                cols = slice(j * P, (j + 1) * P)
+                s_ps = ps_s.tile([P, NI], F32, name="s_ps")
+                nc.tensor.matmul_mx(
+                    out=s_ps[:],
+                    lhsT=uc[:, cols].bitcast(FP8X4),
+                    lhsT_scale=us[:, cols],
+                    rhs=itc[:].bitcast(FP8X4),
+                    rhs_scale=its[:],
+                    start=True,
+                    stop=True,
+                )
+                nc.vector.tensor_scalar(
+                    out=o[:, pr["j0"] % HALF + j, :],
+                    in0=s_ps[:],
+                    scalar1=CLAMP_MIN,
+                    scalar2=CLAMP_MAX,
+                    op0=ALU.max,
+                    op1=ALU.min,
+                )
+            if pr["j0"] % HALF == HALF - 2:
+                nc.sync.dma_start(out=out_v[g, hh], in_=o[:])
+
+        stages = [stage_a, stage_b, stage_c, stage_d]
+        n_pairs = len(pairs)
+        for n in range(n_pairs + len(stages) - 1):
+            for lag in reversed(range(len(stages))):
+                i = n - lag
+                if 0 <= i < n_pairs:
+                    stages[lag](pairs[i])

@@ -30,13 +30,38 @@ def tile_net_pb_t_kernel(tc, h_user, h_item, uW2, ub2, iW2, ib2, out):
         const = ctx.enter_context(tc.tile_pool(name="const", bufs=1))
         xpool = ctx.enter_context(tc.tile_pool(name="xpool", bufs=1))
         stage = ctx.enter_context(tc.tile_pool(name="stage", bufs=3))
-        vpool = ctx.enter_context(tc.tile_pool(name="vpool", bufs=6))
-        small = ctx.enter_context(tc.tile_pool(name="small", bufs=4))
+        vpool = ctx.enter_context(tc.tile_pool(name="vpool", bufs=10))
+        small = ctx.enter_context(tc.tile_pool(name="small", bufs=6))
         opool = ctx.enter_context(tc.tile_pool(name="opool", bufs=4))
         ps_h = ctx.enter_context(tc.psum_pool(name="ps_h", bufs=2))
         ps_u = ctx.enter_context(tc.psum_pool(name="ps_u", bufs=2))
         ps_t = ctx.enter_context(tc.psum_pool(name="ps_t", bufs=2))
         ps_s = ctx.enter_context(tc.psum_pool(name="ps_s", bufs=2))
+        ctx.enter_context(tc.manual_schedule())
+
+        n_groups = NU // (P * GROUP)
+        rows = P * GROUP
+        xi = xpool.tile([P, NI // P, D], BF16, name="xi")
+        nc.sync.dma_start(out=xi[:], in_=h_item.rearrange("(j p) k -> p j k", p=P))
+        raw_i = const.tile([P, 4, D], BF16, name="raw_i")
+        raw_u = const.tile([P, 4, D], BF16, name="raw_u")
+        for raw, w in ((raw_i, iW2), (raw_u, uW2)):
+            nc.sync.dma_start(
+                out=raw[:].rearrange("q (u e) c -> q u e c", u=2),
+                in_=w.rearrange("(u q e) c -> q u e c", u=2, e=2),
+            )
+        bias_i = const.tile([P, D], BF16, name="bias_i")
+        nc.scalar.dma_start(out=bias_i[:], in_=ib2.partition_broadcast(P))
+        bias_u = const.tile([P, D], BF16, name="bias_u")
+        nc.scalar.dma_start(out=bias_u[:], in_=ub2.partition_broadcast(P))
+        xs = []
+        for g in range(n_groups):
+            xg = xpool.tile([P, GROUP, D], BF16, name="x%d" % g)
+            nc.sync.dma_start(
+                out=xg[:],
+                in_=h_user[g * rows : (g + 1) * rows, :].rearrange("(p j) k -> p j k", j=GROUP),
+            )
+            xs.append(xg)
 
         one = const.tile([P, 1], F32, name="one")
         nc.vector.memset(one[:], 1.0)
@@ -48,48 +73,17 @@ def tile_net_pb_t_kernel(tc, h_user, h_item, uW2, ub2, iW2, ib2, out):
         ident_b = const.tile([P, P], BF16, name="ident_b")
         make_identity(nc, ident_b[:])
 
-        xi = xpool.tile([P, NI // P, D], BF16, name="xi")
-        nc.sync.dma_start(out=xi[:], in_=h_item.rearrange("(j p) k -> p j k", p=P))
-
-        def load_weight(w, b, nm):
-            raw = const.tile([P, 4, D], BF16, name="raw_" + nm)
-            nc.sync.dma_start(
-                out=raw[:].rearrange("q (u e) c -> q u e c", u=2),
-                in_=w.rearrange("(u q e) c -> q u e c", u=2, e=2),
-            )
-            bb = const.tile([P, D], BF16, name="bias_" + nm)
-            nc.sync.dma_start(out=bb[:], in_=b.partition_broadcast(P))
-            return raw, bb
-
-        raw_i, bias_i = load_weight(iW2, ib2, "i")
-        n_groups = NU // (P * GROUP)
-        xs = []
-        for g in range(n_groups):
-            xg = xpool.tile([P, GROUP, D], BF16, name="x%d" % g)
-            xs.append(xg)
-        rows = P * GROUP
-        nc.sync.dma_start(out=xs[0][:], in_=h_user[0:rows, :].rearrange("(p j) k -> p j k", j=GROUP))
-        raw_u, bias_u = load_weight(uW2, ub2, "u")
-        for g in range(1, n_groups):
-            nc.sync.dma_start(
-                out=xs[g][:],
-                in_=h_user[g * rows : (g + 1) * rows, :].rearrange("(p j) k -> p j k", j=GROUP),
-            )
-
-        def quantise_weight(raw, nm):
-            grouped = const.tile([P, D, 4], BF16, name="wg_" + nm, align_bytes=64)
-            nc.vector.tensor_copy(out=grouped[:], in_=raw[:].rearrange("p t c -> p c t"))
-            codes = const.tile([P, D], U32, name="wc_" + nm, align_bytes=64)
-            scales = const.tile([P, D], U8, name="ws_" + nm, align_bytes=64)
-            nc.vector.quantize_mx(
-                out=codes[:].bitcast(FP8X4),
-                scales=scales[:],
-                in_=grouped[:].rearrange("p c t -> p (c t)"),
-            )
-            return codes, scales
-
-        wc_i, ws_i = quantise_weight(raw_i, "i")
-        wc_u, ws_u = quantise_weight(raw_u, "u")
+        wg_i = const.tile([P, D, 4], BF16, name="wg_i", align_bytes=64)
+        nc.vector.tensor_copy(out=wg_i[:], in_=raw_i[:].rearrange("p t c -> p c t"))
+        wg_u = const.tile([P, D, 4], BF16, name="wg_u", align_bytes=64)
+        nc.gpsimd.tensor_scalar(
+            out=wg_u[:], in0=raw_u[:].rearrange("p t c -> p c t"), scalar1=1.0, scalar2=0.0, op0=ALU.mult, op1=ALU.add
+        )
+        wc_i = const.tile([P, D], U32, name="wc_i", align_bytes=64)
+        ws_i = const.tile([P, D], U8, name="ws_i", align_bytes=64)
+        wc_u = const.tile([P, D], U32, name="wc_u", align_bytes=64)
+        ws_u = const.tile([P, D], U8, name="ws_u", align_bytes=64)
+        nc.vector.quantize_mx(out=wc_i[:].bitcast(FP8X4), scales=ws_i[:], in_=wg_i[:].rearrange("p c t -> p (c t)"))
 
         itc = const.tile([P, NI], U32, name="itc", align_bytes=64)
         its = const.tile([P, NI], U8, name="its", align_bytes=64)
@@ -98,78 +92,102 @@ def tile_net_pb_t_kernel(tc, h_user, h_item, uW2, ub2, iW2, ib2, out):
 
         pairs = []
         for k in range(NI // (2 * P)):
-            pairs.append({"x": xi, "j0": 2 * k, "wc": wc_i, "ws": ws_i, "bias": bias_i, "item": k})
+            pairs.append({"x": xi, "j0": 2 * k, "wc": wc_i, "ws": ws_i, "bias": bias_i, "item": k, "v": [], "un": [], "u": [], "s": []})
         for g in range(n_groups):
             for k in range(GROUP // 2):
-                pairs.append({"x": xs[g], "j0": 2 * k, "wc": wc_u, "ws": ws_u, "bias": bias_u, "item": None, "g": g})
+                pairs.append({"x": xs[g], "j0": 2 * k, "wc": wc_u, "ws": ws_u, "bias": bias_u, "item": None, "g": g, "v": [], "un": [], "u": [], "s": []})
+        n_pairs = len(pairs)
         o_tiles = {}
 
-        def stage_a(pr):
+        def op_t1(pr):
             hT = ps_h.tile([P, 2, 2, P], F32, name="hT")
             for j in range(2):
                 xw = pr["x"][:, pr["j0"] + j, :].bitcast(F32)
                 for u in range(2):
                     nc.tensor.transpose(hT[:, j, u, :], xw[:, u * P : (u + 1) * P], ident_f[:])
+            pr["hT"] = hT
+
+        def op_cp1(pr):
             hg = stage.tile([P, 2 * D], BF16, name="hg", align_bytes=64)
             nc.scalar.copy(
                 out=hg[:].bitcast(F32).rearrange("p (j r u) -> p j r u", j=2, u=2),
-                in_=hT[:].rearrange("p j u r -> p j r u"),
+                in_=pr["hT"][:].rearrange("p j u r -> p j r u"),
             )
             pr["hg"] = hg
 
-        def stage_b(pr):
+        def op_q1(pr):
             hc = stage.tile([P, 2 * P], U32, name="hc", align_bytes=64)
             hs = stage.tile([P, 2 * P], U8, name="hs", align_bytes=64)
             nc.vector.quantize_mx(out=hc[:].bitcast(FP8X4), scales=hs[:], in_=pr["hg"][:])
-            ss = small.tile([P, 2], F32, name="ss")
-            pr["v"] = []
-            for j in range(2):
-                cols = slice(j * P, (j + 1) * P)
-                u_ps = ps_u.tile([P, D], F32, name="u_ps")
-                nc.tensor.matmul_mx(
-                    out=u_ps[:],
-                    lhsT=hc[:, cols].bitcast(FP8X4),
-                    lhsT_scale=hs[:, cols],
-                    rhs=pr["wc"][:].bitcast(FP8X4),
-                    rhs_scale=pr["ws"][:],
-                    start=True,
-                    stop=True,
-                )
-                v = vpool.tile([P, D], F32, name="v")
-                nc.vector.tensor_tensor(out=v[:], in0=u_ps[:], in1=pr["bias"][:], op=ALU.add)
-                junk = stage.tile([P, D], BF16, name="junk")
-                nc.scalar.activation(out=junk[:], in_=v[:], func=ACTF.Square, accum_out=ss[:, j : j + 1])
-                pr["v"].append(v)
+            pr["hc"] = hc
+            pr["hs"] = hs
+
+        def op_a(pr, j):
+            cols = slice(j * P, (j + 1) * P)
+            u_ps = ps_u.tile([P, D], F32, name="u_ps")
+            nc.tensor.matmul_mx(
+                out=u_ps[:],
+                lhsT=pr["hc"][:, cols].bitcast(FP8X4),
+                lhsT_scale=pr["hs"][:, cols],
+                rhs=pr["wc"][:].bitcast(FP8X4),
+                rhs_scale=pr["ws"][:],
+                start=True,
+                stop=True,
+            )
+            pr["u"].append(u_ps)
+
+        def op_e(pr, j):
+            v = vpool.tile([P, D], F32, name="v")
+            nc.vector.tensor_tensor(out=v[:], in0=pr["u"][j][:], in1=pr["bias"][:], op=ALU.add)
+            pr["v"].append(v)
+
+        def op_f(pr, j):
+            if j == 0:
+                ss = small.tile([P, 2], F32, name="ss")
+                pr["ss"] = ss
+            junk = stage.tile([P, D], BF16, name="junk")
+            nc.scalar.activation(out=junk[:], in_=pr["v"][j][:], func=ACTF.Square, accum_out=pr["ss"][:, j : j + 1])
+
+        def op_sqrt(pr):
             nrm = small.tile([P, 2], F32, name="nrm")
-            nc.scalar.activation(out=nrm[:], in_=ss[:], func=ACTF.Sqrt)
+            nc.scalar.activation(out=nrm[:], in_=pr["ss"][:], func=ACTF.Sqrt)
+            pr["nrm"] = nrm
+
+        def op_g(pr):
             nrc = small.tile([P, 2], F32, name="nrc")
-            nc.vector.tensor_scalar_max(out=nrc[:], in0=nrm[:], scalar1=EPS_NORM)
+            nc.vector.tensor_scalar_max(out=nrc[:], in0=pr["nrm"][:], scalar1=EPS_NORM)
             rn = small.tile([P, 2], F32, name="rn")
             nc.vector.reciprocal(out=rn[:], in_=nrc[:])
             pr["rn"] = rn
 
-        def stage_c(pr):
+        def op_h(pr, j):
+            un = vpool.tile([P, D], BF16, name="un")
+            nc.gpsimd.tensor_scalar(
+                out=un[:],
+                in0=pr["v"][j][:],
+                scalar1=pr["rn"][:, j : j + 1],
+                scalar2=0.0,
+                op0=ALU.mult,
+                op1=ALU.add,
+            )
+            pr["un"].append(un)
+
+        def op_t2(pr):
             unT = ps_t.tile([P, 2, 4, P], BF16, name="unT")
             for j in range(2):
-                un = vpool.tile([P, D], BF16, name="un")
-                nc.gpsimd.tensor_scalar(
-                    out=un[:],
-                    in0=pr["v"][j][:],
-                    scalar1=pr["rn"][:, j : j + 1],
-                    scalar2=0.0,
-                    op0=ALU.mult,
-                    op1=ALU.add,
-                )
                 for t in range(4):
-                    nc.tensor.transpose(unT[:, j, t, :], un[:, t * P : (t + 1) * P], ident_b[:])
+                    nc.tensor.transpose(unT[:, j, t, :], pr["un"][j][:, t * P : (t + 1) * P], ident_b[:])
+            pr["unT"] = unT
+
+        def op_j(pr):
             ug = stage.tile([P, 2 * D], BF16, name="ug", align_bytes=64)
             nc.scalar.copy(
                 out=ug[:].rearrange("p (j r t) -> p j r t", j=2, t=4),
-                in_=unT[:].rearrange("p j t r -> p j r t"),
+                in_=pr["unT"][:].rearrange("p j t r -> p j r t"),
             )
             pr["ug"] = ug
 
-        def stage_d(pr):
+        def op_q2(pr):
             if pr["item"] is not None:
                 cols = slice(pr["item"] * 2 * P, (pr["item"] + 1) * 2 * P)
                 nc.vector.quantize_mx(out=itc[:, cols].bitcast(FP8X4), scales=its[:, cols], in_=pr["ug"][:])
@@ -177,39 +195,72 @@ def tile_net_pb_t_kernel(tc, h_user, h_item, uW2, ub2, iW2, ib2, out):
             uc = stage.tile([P, 2 * P], U32, name="uc", align_bytes=64)
             us = stage.tile([P, 2 * P], U8, name="us", align_bytes=64)
             nc.vector.quantize_mx(out=uc[:].bitcast(FP8X4), scales=us[:], in_=pr["ug"][:])
+            pr["uc"] = uc
+            pr["us"] = us
+
+        def op_c(pr, j):
+            if pr["item"] is not None:
+                return
+            cols = slice(j * P, (j + 1) * P)
+            s_ps = ps_s.tile([P, NI], F32, name="s_ps")
+            nc.tensor.matmul_mx(
+                out=s_ps[:],
+                lhsT=pr["uc"][:, cols].bitcast(FP8X4),
+                lhsT_scale=pr["us"][:, cols],
+                rhs=itc[:].bitcast(FP8X4),
+                rhs_scale=its[:],
+                start=True,
+                stop=True,
+            )
+            pr["s"].append(s_ps)
+
+        def op_m(pr, j):
+            if pr["item"] is not None:
+                return
             g = pr["g"]
             hh = pr["j0"] // HALF
-            if pr["j0"] % HALF == 0:
+            jj = pr["j0"] % HALF + j
+            if jj == 0:
                 o_new = opool.tile([P, HALF, NI], F32, name="o")
                 o_tiles[(g, hh)] = o_new
             o = o_tiles[(g, hh)]
-            for j in range(2):
-                cols = slice(j * P, (j + 1) * P)
-                s_ps = ps_s.tile([P, NI], F32, name="s_ps")
-                nc.tensor.matmul_mx(
-                    out=s_ps[:],
-                    lhsT=uc[:, cols].bitcast(FP8X4),
-                    lhsT_scale=us[:, cols],
-                    rhs=itc[:].bitcast(FP8X4),
-                    rhs_scale=its[:],
-                    start=True,
-                    stop=True,
-                )
-                nc.vector.tensor_scalar(
-                    out=o[:, pr["j0"] % HALF + j, :],
-                    in0=s_ps[:],
-                    scalar1=CLAMP_MIN,
-                    scalar2=CLAMP_MAX,
-                    op0=ALU.max,
-                    op1=ALU.min,
-                )
-            if pr["j0"] % HALF == HALF - 2:
+            nc.vector.tensor_scalar(
+                out=o[:, jj, :],
+                in0=pr["s"][j][:],
+                scalar1=CLAMP_MIN,
+                scalar2=CLAMP_MAX,
+                op0=ALU.max,
+                op1=ALU.min,
+            )
+            if jj == HALF - 1:
                 nc.sync.dma_start(out=out_v[g, hh], in_=o[:])
 
-        stages = [stage_a, stage_b, stage_c, stage_d]
-        n_pairs = len(pairs)
-        for n in range(n_pairs + len(stages) - 1):
-            for lag in reversed(range(len(stages))):
-                i = n - lag
-                if 0 <= i < n_pairs:
-                    stages[lag](pairs[i])
+        def at(i, fn, *args):
+            if 0 <= i < n_pairs:
+                fn(pairs[i], *args)
+
+        for n in range(-4, n_pairs + 6):
+            if n == 0:
+                nc.vector.quantize_mx(
+                    out=wc_u[:].bitcast(FP8X4), scales=ws_u[:], in_=wg_u[:].rearrange("p c t -> p (c t)")
+                )
+            at(n, op_e, 0)
+            at(n, op_e, 1)
+            at(n + 2, op_q1)
+            at(n - 2, op_g)
+            at(n - 5, op_q2)
+            at(n - 6, op_m, 0)
+            at(n - 6, op_m, 1)
+            at(n - 2, op_h, 0)
+            at(n - 2, op_h, 1)
+            at(n + 1, op_a, 0)
+            at(n + 1, op_a, 1)
+            at(n - 3, op_t2)
+            at(n + 4, op_t1)
+            at(n - 5, op_c, 0)
+            at(n - 5, op_c, 1)
+            at(n - 1, op_f, 0)
+            at(n - 1, op_f, 1)
+            at(n - 1, op_sqrt)
+            at(n + 3, op_cp1)
+            at(n - 4, op_j)

@@ -45,11 +45,14 @@ def tile_net_pb_t_kernel(tc, h_user, h_item, uW2, ub2, iW2, ib2, out):
         nc.sync.dma_start(out=xi[:], in_=h_item.rearrange("(j p) k -> p j k", p=P))
         raw_i = const.tile([P, 4, D], BF16, name="raw_i")
         raw_u = const.tile([P, 4, D], BF16, name="raw_u")
-        for raw, w in ((raw_i, iW2), (raw_u, uW2)):
+
+        def load_weight(raw, w):
             nc.sync.dma_start(
                 out=raw[:].rearrange("q (u e) c -> q u e c", u=2),
                 in_=w.rearrange("(u q e) c -> q u e c", u=2, e=2),
             )
+
+        load_weight(raw_i, iW2)
         bias_i = const.tile([P, D], BF16, name="bias_i")
         nc.scalar.dma_start(out=bias_i[:], in_=ib2.partition_broadcast(P))
         bias_u = const.tile([P, D], BF16, name="bias_u")
@@ -62,6 +65,8 @@ def tile_net_pb_t_kernel(tc, h_user, h_item, uW2, ub2, iW2, ib2, out):
                 in_=h_user[g * rows : (g + 1) * rows, :].rearrange("(p j) k -> p j k", j=GROUP),
             )
             xs.append(xg)
+            if g == 0:
+                load_weight(raw_u, uW2)
 
         one = const.tile([P, 1], F32, name="one")
         nc.vector.memset(one[:], 1.0)
@@ -153,11 +158,14 @@ def tile_net_pb_t_kernel(tc, h_user, h_item, uW2, ub2, iW2, ib2, out):
             nc.scalar.activation(out=nrm[:], in_=pr["ss"][:], func=ACTF.Sqrt)
             pr["nrm"] = nrm
 
-        def op_g(pr):
+        def op_max(pr):
             nrc = small.tile([P, 2], F32, name="nrc")
             nc.vector.tensor_scalar_max(out=nrc[:], in0=pr["nrm"][:], scalar1=EPS_NORM)
+            pr["nrc"] = nrc
+
+        def op_rec(pr):
             rn = small.tile([P, 2], F32, name="rn")
-            nc.vector.reciprocal(out=rn[:], in_=nrc[:])
+            nc.vector.reciprocal(out=rn[:], in_=pr["nrc"][:])
             pr["rn"] = rn
 
         def op_h(pr, j):
@@ -232,7 +240,10 @@ def tile_net_pb_t_kernel(tc, h_user, h_item, uW2, ub2, iW2, ib2, out):
                 op0=ALU.max,
                 op1=ALU.min,
             )
-            if jj == HALF - 1:
+            last = g == n_groups - 1 and hh == GROUP // HALF - 1
+            if last and jj % 2 == 1:
+                nc.sync.dma_start(out=out_v[g, hh][:, jj - 1 : jj + 1, :], in_=o[:, jj - 1 : jj + 1, :])
+            elif jj == HALF - 1:
                 nc.sync.dma_start(out=out_v[g, hh], in_=o[:])
 
         def at(i, fn, *args):
@@ -240,17 +251,18 @@ def tile_net_pb_t_kernel(tc, h_user, h_item, uW2, ub2, iW2, ib2, out):
                 fn(pairs[i], *args)
 
         for n in range(-4, n_pairs + 6):
+            at(n, op_e, 0)
+            at(n, op_e, 1)
+            at(n + 2, op_q1)
+            at(n - 2, op_max)
+            at(n - 5, op_q2)
+            at(n - 2, op_rec)
+            at(n - 6, op_m, 0)
+            at(n - 6, op_m, 1)
             if n == 0:
                 nc.vector.quantize_mx(
                     out=wc_u[:].bitcast(FP8X4), scales=ws_u[:], in_=wg_u[:].rearrange("p c t -> p (c t)")
                 )
-            at(n, op_e, 0)
-            at(n, op_e, 1)
-            at(n + 2, op_q1)
-            at(n - 2, op_g)
-            at(n - 5, op_q2)
-            at(n - 6, op_m, 0)
-            at(n - 6, op_m, 1)
             at(n - 2, op_h, 0)
             at(n - 2, op_h, 1)
             at(n + 1, op_a, 0)
@@ -261,6 +273,6 @@ def tile_net_pb_t_kernel(tc, h_user, h_item, uW2, ub2, iW2, ib2, out):
             at(n - 5, op_c, 1)
             at(n - 1, op_f, 0)
             at(n - 1, op_f, 1)
-            at(n - 1, op_sqrt)
             at(n + 3, op_cp1)
+            at(n - 1, op_sqrt)
             at(n - 4, op_j)

@@ -22,6 +22,7 @@ CLAMP_MIN = 1e-6
 CLAMP_MAX = 1.0
 
 FLOPS = 2 * NU * D * D + 2 * NI * D * D + 2 * NU * D * NI
+W_SPLIT = 336
 
 
 def tile_net_pb_t_kernel(tc, h_user, h_item, uW2, ub2, iW2, ib2, out):
@@ -39,10 +40,26 @@ def tile_net_pb_t_kernel(tc, h_user, h_item, uW2, ub2, iW2, ib2, out):
         ps_s = ctx.enter_context(tc.psum_pool(name="ps_s", bufs=2))
         ctx.enter_context(tc.manual_schedule())
 
+        brow = const.tile([P, 2, D], BF16, name="brow")
+        nc.vector.memset(brow[:], 0.0)
+        ones = const.tile([P, P], BF16, name="ones")
+        nc.vector.memset(ones[:], 1.0)
+        one = const.tile([P, 1], F32, name="one")
+        nc.vector.memset(one[:], 1.0)
+        ident_f = const.tile([P, P], F32, name="ident_f")
+        make_identity(nc, ident_f[:])
+        ident_b = const.tile([P, P], BF16, name="ident_b")
+        make_identity(nc, ident_b[:])
+
+        nc.scalar.dma_start(out=brow[0:1, 0, :], in_=ib2.unsqueeze(0))
+        nc.scalar.dma_start(out=brow[0:1, 1, :], in_=ub2.unsqueeze(0))
+        warm = const.tile([P, 1], F32, name="warm")
+        nc.scalar.activation(out=warm[:], in_=one[:], func=ACTF.Sqrt)
+
         n_groups = NU // (P * GROUP)
         rows = P * GROUP
         xi = xpool.tile([P, NI // P, D], BF16, name="xi")
-        nc.sync.dma_start(out=xi[:], in_=h_item.rearrange("(j p) k -> p j k", p=P))
+        hi_v = h_item.rearrange("(j p) k -> p j k", p=P)
         raw_i = const.tile([P, 4, D], BF16, name="raw_i")
         raw_u = const.tile([P, 4, D], BF16, name="raw_u")
 
@@ -52,11 +69,9 @@ def tile_net_pb_t_kernel(tc, h_user, h_item, uW2, ub2, iW2, ib2, out):
                 in_=w.rearrange("(u q e) c -> q u e c", u=2, e=2),
             )
 
+        nc.sync.dma_start(out=xi[:, 0:2, :], in_=hi_v[:, 0:2, :])
         load_weight(raw_i, iW2)
-        bias_i = const.tile([P, D], BF16, name="bias_i")
-        nc.scalar.dma_start(out=bias_i[:], in_=ib2.partition_broadcast(P))
-        bias_u = const.tile([P, D], BF16, name="bias_u")
-        nc.scalar.dma_start(out=bias_u[:], in_=ub2.partition_broadcast(P))
+        nc.sync.dma_start(out=xi[:, 2:4, :], in_=hi_v[:, 2:4, :])
         xs = []
         for g in range(n_groups):
             xg = xpool.tile([P, GROUP, D], BF16, name="x%d" % g)
@@ -68,18 +83,17 @@ def tile_net_pb_t_kernel(tc, h_user, h_item, uW2, ub2, iW2, ib2, out):
             if g == 0:
                 load_weight(raw_u, uW2)
 
-        one = const.tile([P, 1], F32, name="one")
-        nc.vector.memset(one[:], 1.0)
-        warm = const.tile([P, 1], F32, name="warm")
-        nc.scalar.activation(out=warm[:], in_=one[:], func=ACTF.Sqrt)
-
-        ident_f = const.tile([P, P], F32, name="ident_f")
-        make_identity(nc, ident_f[:])
-        ident_b = const.tile([P, P], BF16, name="ident_b")
-        make_identity(nc, ident_b[:])
+        biases = []
+        for k in range(2):
+            b_ps = ps_u.tile([P, D], F32, name="u_ps")
+            nc.tensor.matmul(out=b_ps[:], lhsT=ones[:], rhs=brow[:, k, :], start=True, stop=True)
+            b_sb = const.tile([P, D], F32, name="bias%d" % k)
+            nc.vector.tensor_copy(out=b_sb[:], in_=b_ps[:])
+            biases.append(b_sb)
+        bias_i, bias_u = biases
 
         wg_i = const.tile([P, D, 4], BF16, name="wg_i", align_bytes=64)
-        nc.vector.tensor_copy(out=wg_i[:], in_=raw_i[:].rearrange("p t c -> p c t"))
+        nc.vector.tensor_copy(out=wg_i[:, 0:W_SPLIT, :], in_=raw_i[:, :, 0:W_SPLIT].rearrange("p t c -> p c t"))
         wg_u = const.tile([P, D, 4], BF16, name="wg_u", align_bytes=64)
         nc.gpsimd.tensor_scalar(
             out=wg_u[:], in0=raw_u[:].rearrange("p t c -> p c t"), scalar1=1.0, scalar2=0.0, op0=ALU.mult, op1=ALU.add
@@ -88,7 +102,6 @@ def tile_net_pb_t_kernel(tc, h_user, h_item, uW2, ub2, iW2, ib2, out):
         ws_i = const.tile([P, D], U8, name="ws_i", align_bytes=64)
         wc_u = const.tile([P, D], U32, name="wc_u", align_bytes=64)
         ws_u = const.tile([P, D], U8, name="ws_u", align_bytes=64)
-        nc.vector.quantize_mx(out=wc_i[:].bitcast(FP8X4), scales=ws_i[:], in_=wg_i[:].rearrange("p c t -> p (c t)"))
 
         itc = const.tile([P, NI], U32, name="itc", align_bytes=64)
         its = const.tile([P, NI], U8, name="its", align_bytes=64)
@@ -103,7 +116,6 @@ def tile_net_pb_t_kernel(tc, h_user, h_item, uW2, ub2, iW2, ib2, out):
                 pairs.append({"x": xs[g], "j0": 2 * k, "wc": wc_u, "ws": ws_u, "bias": bias_u, "item": None, "g": g, "v": [], "un": [], "u": [], "s": []})
         n_pairs = len(pairs)
         o_tiles = {}
-
         def op_t1(pr):
             hT = ps_h.tile([P, 2, 2, P], F32, name="hT")
             for j in range(2):
@@ -158,14 +170,14 @@ def tile_net_pb_t_kernel(tc, h_user, h_item, uW2, ub2, iW2, ib2, out):
             nc.scalar.activation(out=nrm[:], in_=pr["ss"][:], func=ACTF.Sqrt)
             pr["nrm"] = nrm
 
-        def op_max(pr):
-            nrc = small.tile([P, 2], F32, name="nrc")
-            nc.vector.tensor_scalar_max(out=nrc[:], in0=pr["nrm"][:], scalar1=EPS_NORM)
-            pr["nrc"] = nrc
-
         def op_rec(pr):
+            rcp = small.tile([P, 2], F32, name="rcp")
+            nc.vector.reciprocal(out=rcp[:], in_=pr["nrm"][:])
+            pr["rcp"] = rcp
+
+        def op_min(pr):
             rn = small.tile([P, 2], F32, name="rn")
-            nc.vector.reciprocal(out=rn[:], in_=pr["nrc"][:])
+            nc.gpsimd.tensor_scalar_min(out=rn[:], in0=pr["rcp"][:], scalar1=1.0 / EPS_NORM)
             pr["rn"] = rn
 
         def op_h(pr, j):
@@ -241,8 +253,10 @@ def tile_net_pb_t_kernel(tc, h_user, h_item, uW2, ub2, iW2, ib2, out):
                 op1=ALU.min,
             )
             last = g == n_groups - 1 and hh == GROUP // HALF - 1
-            if last and jj % 2 == 1:
-                nc.sync.dma_start(out=out_v[g, hh][:, jj - 1 : jj + 1, :], in_=o[:, jj - 1 : jj + 1, :])
+            if last and jj == 1:
+                nc.sync.dma_start(out=out_v[g, hh][:, 0:2, :], in_=o[:, 0:2, :])
+            elif last and jj >= 2:
+                nc.sync.dma_start(out=out_v[g, hh][:, jj : jj + 1, :], in_=o[:, jj : jj + 1, :])
             elif jj == HALF - 1:
                 nc.sync.dma_start(out=out_v[g, hh], in_=o[:])
 
@@ -254,15 +268,19 @@ def tile_net_pb_t_kernel(tc, h_user, h_item, uW2, ub2, iW2, ib2, out):
             at(n, op_e, 0)
             at(n, op_e, 1)
             at(n + 2, op_q1)
-            at(n - 2, op_max)
             at(n - 5, op_q2)
             at(n - 2, op_rec)
             at(n - 6, op_m, 0)
             at(n - 6, op_m, 1)
+            if n == -2:
+                nc.vector.quantize_mx(
+                    out=wc_i[:].bitcast(FP8X4), scales=ws_i[:], in_=wg_i[:].rearrange("p c t -> p (c t)")
+                )
             if n == 0:
                 nc.vector.quantize_mx(
                     out=wc_u[:].bitcast(FP8X4), scales=ws_u[:], in_=wg_u[:].rearrange("p c t -> p (c t)")
                 )
+            at(n - 2, op_min)
             at(n - 2, op_h, 0)
             at(n - 2, op_h, 1)
             at(n + 1, op_a, 0)
@@ -276,3 +294,5 @@ def tile_net_pb_t_kernel(tc, h_user, h_item, uW2, ub2, iW2, ib2, out):
             at(n + 3, op_cp1)
             at(n - 1, op_sqrt)
             at(n - 4, op_j)
+            if n == -3:
+                nc.scalar.copy(out=wg_i[:, W_SPLIT:D, :], in_=raw_i[:, :, W_SPLIT:D].rearrange("p t c -> p c t"))

@@ -51,8 +51,6 @@ def tile_net_pb_t_kernel(tc, h_user, h_item, uW2, ub2, iW2, ib2, out):
         ident_b = const.tile([P, P], BF16, name="ident_b")
         make_identity(nc, ident_b[:])
 
-        nc.scalar.dma_start(out=brow[0:1, 0, :], in_=ib2.unsqueeze(0))
-        nc.scalar.dma_start(out=brow[0:1, 1, :], in_=ub2.unsqueeze(0))
         warm = const.tile([P, 1], F32, name="warm")
         nc.scalar.activation(out=warm[:], in_=one[:], func=ACTF.Sqrt)
 
@@ -71,26 +69,30 @@ def tile_net_pb_t_kernel(tc, h_user, h_item, uW2, ub2, iW2, ib2, out):
 
         nc.sync.dma_start(out=xi[:, 0:2, :], in_=hi_v[:, 0:2, :])
         load_weight(raw_i, iW2)
+        nc.sync.dma_start(out=brow[0:1, 0, :], in_=ib2.unsqueeze(0))
+        nc.sync.dma_start(out=brow[0:1, 1, :], in_=ub2.unsqueeze(0))
         nc.sync.dma_start(out=xi[:, 2:4, :], in_=hi_v[:, 2:4, :])
         xs = []
         for g in range(n_groups):
             xg = xpool.tile([P, GROUP, D], BF16, name="x%d" % g)
-            nc.sync.dma_start(
-                out=xg[:],
-                in_=h_user[g * rows : (g + 1) * rows, :].rearrange("(p j) k -> p j k", j=GROUP),
-            )
-            xs.append(xg)
+            src = h_user[g * rows : (g + 1) * rows, :].rearrange("(p j) k -> p j k", j=GROUP)
             if g == 0:
+                nc.sync.dma_start(out=xg[:, 0:HALF, :], in_=src[:, 0:HALF, :])
                 load_weight(raw_u, uW2)
+                nc.sync.dma_start(out=xg[:, HALF:GROUP, :], in_=src[:, HALF:GROUP, :])
+            else:
+                nc.sync.dma_start(out=xg[:], in_=src)
+            xs.append(xg)
 
-        biases = []
-        for k in range(2):
-            b_ps = ps_u.tile([P, D], F32, name="u_ps")
-            nc.tensor.matmul(out=b_ps[:], lhsT=ones[:], rhs=brow[:, k, :], start=True, stop=True)
-            b_sb = const.tile([P, D], F32, name="bias%d" % k)
-            nc.vector.tensor_copy(out=b_sb[:], in_=b_ps[:])
-            biases.append(b_sb)
-        bias_i, bias_u = biases
+        bias_i = const.tile([P, D], F32, name="bias_i")
+        bias_u = const.tile([P, D], F32, name="bias_u")
+        bias_ps = []
+
+        def spread_biases():
+            for k in range(2):
+                b_ps = ps_u.tile([P, D], F32, name="u_ps")
+                nc.tensor.matmul(out=b_ps[:], lhsT=ones[:], rhs=brow[:, k, :], start=True, stop=True)
+                bias_ps.append(b_ps)
 
         wg_i = const.tile([P, D, 4], BF16, name="wg_i", align_bytes=64)
         nc.vector.tensor_copy(out=wg_i[:, 0:W_SPLIT, :], in_=raw_i[:, :, 0:W_SPLIT].rearrange("p t c -> p c t"))
@@ -276,7 +278,10 @@ def tile_net_pb_t_kernel(tc, h_user, h_item, uW2, ub2, iW2, ib2, out):
                 nc.vector.quantize_mx(
                     out=wc_i[:].bitcast(FP8X4), scales=ws_i[:], in_=wg_i[:].rearrange("p c t -> p (c t)")
                 )
-            if n == 0:
+                spread_biases()
+                nc.vector.tensor_copy(out=bias_i[:], in_=bias_ps[0][:])
+                nc.vector.tensor_copy(out=bias_u[:], in_=bias_ps[1][:])
+            if n == 1:
                 nc.vector.quantize_mx(
                     out=wc_u[:].bitcast(FP8X4), scales=ws_u[:], in_=wg_u[:].rearrange("p c t -> p (c t)")
                 )
@@ -286,7 +291,10 @@ def tile_net_pb_t_kernel(tc, h_user, h_item, uW2, ub2, iW2, ib2, out):
             at(n + 1, op_a, 0)
             at(n + 1, op_a, 1)
             at(n - 3, op_t2)
-            at(n + 4, op_t1)
+            if n == -1:
+                at(2, op_t1)
+            if n != -2:
+                at(n + 4, op_t1)
             at(n - 5, op_c, 0)
             at(n - 5, op_c, 1)
             at(n - 1, op_f, 0)

@@ -48,8 +48,6 @@ def tile_net_pb_t_kernel(tc, h_user, h_item, uW2, ub2, iW2, ib2, out):
         nc.vector.memset(one[:], 1.0)
         ident_f = const.tile([P, P], F32, name="ident_f")
         make_identity(nc, ident_f[:])
-        ident_b = const.tile([P, P], BF16, name="ident_b")
-        make_identity(nc, ident_b[:])
 
         warm = const.tile([P, 1], F32, name="warm")
         nc.scalar.activation(out=warm[:], in_=one[:], func=ACTF.Sqrt)
@@ -195,17 +193,18 @@ def tile_net_pb_t_kernel(tc, h_user, h_item, uW2, ub2, iW2, ib2, out):
             pr["un"].append(un)
 
         def op_t2(pr):
-            unT = ps_t.tile([P, 2, 4, P], BF16, name="unT")
+            unT = ps_t.tile([P, 2, 2, P], F32, name="unT")
             for j in range(2):
-                for t in range(4):
-                    nc.tensor.transpose(unT[:, j, t, :], pr["un"][j][:, t * P : (t + 1) * P], ident_b[:])
+                uw = pr["un"][j][:].bitcast(F32)
+                for u in range(2):
+                    nc.tensor.transpose(unT[:, j, u, :], uw[:, u * P : (u + 1) * P], ident_f[:])
             pr["unT"] = unT
 
         def op_j(pr):
             ug = stage.tile([P, 2 * D], BF16, name="ug", align_bytes=64)
             nc.scalar.copy(
-                out=ug[:].rearrange("p (j r t) -> p j r t", j=2, t=4),
-                in_=pr["unT"][:].rearrange("p j t r -> p j r t"),
+                out=ug[:].bitcast(F32).rearrange("p (j r u) -> p j r u", j=2, u=2),
+                in_=pr["unT"][:].rearrange("p j u r -> p j r u"),
             )
             pr["ug"] = ug
 

@@ -50,7 +50,7 @@ def tile_net_pb_t_kernel(tc, h_user, h_item, uW2, ub2, iW2, ib2, out):
         make_identity(nc, ident_f[:])
 
         warm = const.tile([P, 1], F32, name="warm")
-        nc.scalar.activation(out=warm[:], in_=one[:], func=ACTF.Sqrt)
+        nc.scalar.activation(out=warm[:], in_=one[:], func=ACTF.Abs_reciprocal_sqrt)
 
         n_groups = NU // (P * GROUP)
         rows = P * GROUP
@@ -124,20 +124,43 @@ def tile_net_pb_t_kernel(tc, h_user, h_item, uW2, ub2, iW2, ib2, out):
                     nc.tensor.transpose(hT[:, j, u, :], xw[:, u * P : (u + 1) * P], ident_f[:])
             pr["hT"] = hT
 
-        def op_cp1(pr):
-            hg = stage.tile([P, 2 * D], BF16, name="hg", align_bytes=64)
+        grouped = {}
+
+        def op_group(n):
+            if 0 <= n + 3 < n_pairs or 0 <= n - 4 < n_pairs:
+                g_new = stage.tile([P, 4 * D], BF16, name="gt", align_bytes=64)
+                grouped[n] = g_new
+
+        def op_cp1(pr, n):
             nc.scalar.copy(
-                out=hg[:].bitcast(F32).rearrange("p (j r u) -> p j r u", j=2, u=2),
+                out=grouped[n][:, 0 : 2 * D].bitcast(F32).rearrange("p (j r u) -> p j r u", j=2, u=2),
                 in_=pr["hT"][:].rearrange("p j u r -> p j r u"),
             )
-            pr["hg"] = hg
 
-        def op_q1(pr):
-            hc = stage.tile([P, 2 * P], U32, name="hc", align_bytes=64)
-            hs = stage.tile([P, 2 * P], U8, name="hs", align_bytes=64)
-            nc.vector.quantize_mx(out=hc[:].bitcast(FP8X4), scales=hs[:], in_=pr["hg"][:])
-            pr["hc"] = hc
-            pr["hs"] = hs
+        def op_q(n):
+            has_h = 0 <= n + 2 < n_pairs
+            has_u = 0 <= n - 5 < n_pairs
+            if not has_h and not has_u:
+                return
+            gt = grouped[n - 1]
+            item = pairs[n - 5]["item"] if has_u else None
+            if item is not None:
+                cols = slice(item * 2 * P, (item + 1) * 2 * P)
+                nc.vector.quantize_mx(out=itc[:, cols].bitcast(FP8X4), scales=its[:, cols], in_=gt[:, 2 * D : 4 * D])
+                has_u = False
+            qc = stage.tile([P, 4 * P], U32, name="qc", align_bytes=64)
+            qs = stage.tile([P, 4 * P], U8, name="qs", align_bytes=64)
+            w0 = 0 if has_h else 2 * P
+            w1 = 4 * P if has_u else 2 * P
+            nc.vector.quantize_mx(
+                out=qc[:, w0:w1].bitcast(FP8X4), scales=qs[:, w0:w1], in_=gt[:, 4 * w0 : 4 * w1]
+            )
+            if has_h:
+                pairs[n + 2]["hc"] = qc
+                pairs[n + 2]["hs"] = qs
+            if has_u:
+                pairs[n - 5]["uc"] = qc
+                pairs[n - 5]["us"] = qs
 
         def op_a(pr, j):
             cols = slice(j * P, (j + 1) * P)
@@ -165,19 +188,14 @@ def tile_net_pb_t_kernel(tc, h_user, h_item, uW2, ub2, iW2, ib2, out):
             junk = stage.tile([P, D], BF16, name="junk")
             nc.scalar.activation(out=junk[:], in_=pr["v"][j][:], func=ACTF.Square, accum_out=pr["ss"][:, j : j + 1])
 
-        def op_sqrt(pr):
-            nrm = small.tile([P, 2], F32, name="nrm")
-            nc.scalar.activation(out=nrm[:], in_=pr["ss"][:], func=ACTF.Sqrt)
-            pr["nrm"] = nrm
-
-        def op_rec(pr):
+        def op_rsqrt(pr):
             rcp = small.tile([P, 2], F32, name="rcp")
-            nc.vector.reciprocal(out=rcp[:], in_=pr["nrm"][:])
+            nc.scalar.activation(out=rcp[:], in_=pr["ss"][:], func=ACTF.Abs_reciprocal_sqrt)
             pr["rcp"] = rcp
 
         def op_min(pr):
             rn = small.tile([P, 2], F32, name="rn")
-            nc.gpsimd.tensor_scalar_min(out=rn[:], in0=pr["rcp"][:], scalar1=1.0 / EPS_NORM)
+            nc.vector.tensor_scalar_min(out=rn[:], in0=pr["rcp"][:], scalar1=1.0 / EPS_NORM)
             pr["rn"] = rn
 
         def op_h(pr, j):
@@ -200,29 +218,16 @@ def tile_net_pb_t_kernel(tc, h_user, h_item, uW2, ub2, iW2, ib2, out):
                     nc.tensor.transpose(unT[:, j, u, :], uw[:, u * P : (u + 1) * P], ident_f[:])
             pr["unT"] = unT
 
-        def op_j(pr):
-            ug = stage.tile([P, 2 * D], BF16, name="ug", align_bytes=64)
+        def op_j(pr, n):
             nc.scalar.copy(
-                out=ug[:].bitcast(F32).rearrange("p (j r u) -> p j r u", j=2, u=2),
+                out=grouped[n][:, 2 * D : 4 * D].bitcast(F32).rearrange("p (j r u) -> p j r u", j=2, u=2),
                 in_=pr["unT"][:].rearrange("p j u r -> p j r u"),
             )
-            pr["ug"] = ug
-
-        def op_q2(pr):
-            if pr["item"] is not None:
-                cols = slice(pr["item"] * 2 * P, (pr["item"] + 1) * 2 * P)
-                nc.vector.quantize_mx(out=itc[:, cols].bitcast(FP8X4), scales=its[:, cols], in_=pr["ug"][:])
-                return
-            uc = stage.tile([P, 2 * P], U32, name="uc", align_bytes=64)
-            us = stage.tile([P, 2 * P], U8, name="us", align_bytes=64)
-            nc.vector.quantize_mx(out=uc[:].bitcast(FP8X4), scales=us[:], in_=pr["ug"][:])
-            pr["uc"] = uc
-            pr["us"] = us
 
         def op_c(pr, j):
             if pr["item"] is not None:
                 return
-            cols = slice(j * P, (j + 1) * P)
+            cols = slice((2 + j) * P, (3 + j) * P)
             s_ps = ps_s.tile([P, NI], F32, name="s_ps")
             nc.tensor.matmul_mx(
                 out=s_ps[:],
@@ -268,9 +273,8 @@ def tile_net_pb_t_kernel(tc, h_user, h_item, uW2, ub2, iW2, ib2, out):
         for n in range(-4, n_pairs + 6):
             at(n, op_e, 0)
             at(n, op_e, 1)
-            at(n + 2, op_q1)
-            at(n - 5, op_q2)
-            at(n - 2, op_rec)
+            op_q(n)
+            at(n - 2, op_min)
             at(n - 6, op_m, 0)
             at(n - 6, op_m, 1)
             if n == -2:
@@ -284,7 +288,6 @@ def tile_net_pb_t_kernel(tc, h_user, h_item, uW2, ub2, iW2, ib2, out):
                 nc.vector.quantize_mx(
                     out=wc_u[:].bitcast(FP8X4), scales=ws_u[:], in_=wg_u[:].rearrange("p c t -> p (c t)")
                 )
-            at(n - 2, op_min)
             at(n - 2, op_h, 0)
             at(n - 2, op_h, 1)
             at(n + 1, op_a, 0)
@@ -296,10 +299,11 @@ def tile_net_pb_t_kernel(tc, h_user, h_item, uW2, ub2, iW2, ib2, out):
                 at(n + 4, op_t1)
             at(n - 5, op_c, 0)
             at(n - 5, op_c, 1)
+            op_group(n)
             at(n - 1, op_f, 0)
             at(n - 1, op_f, 1)
-            at(n + 3, op_cp1)
-            at(n - 1, op_sqrt)
-            at(n - 4, op_j)
+            at(n + 3, op_cp1, n)
+            at(n - 1, op_rsqrt)
+            at(n - 4, op_j, n)
             if n == -3:
                 nc.scalar.copy(out=wg_i[:, W_SPLIT:D, :], in_=raw_i[:, :, W_SPLIT:D].rearrange("p t c -> p c t"))

@@ -240,6 +240,11 @@ def tile_net_pb_t_kernel(tc, h_user, h_item, uW2, ub2, iW2, ib2, out):
             )
             pr["s"].append(s_ps)
 
+        def clamp(dst, src):
+            nc.vector.tensor_scalar(
+                out=dst, in0=src, scalar1=CLAMP_MIN, scalar2=CLAMP_MAX, op0=ALU.max, op1=ALU.min
+            )
+
         def op_m(pr, j):
             if pr["item"] is not None:
                 return
@@ -250,30 +255,41 @@ def tile_net_pb_t_kernel(tc, h_user, h_item, uW2, ub2, iW2, ib2, out):
                 o_new = opool.tile([P, HALF, NI], F32, name="o")
                 o_tiles[(g, hh)] = o_new
             o = o_tiles[(g, hh)]
-            nc.vector.tensor_scalar(
-                out=o[:, jj, :],
-                in0=pr["s"][j][:],
-                scalar1=CLAMP_MIN,
-                scalar2=CLAMP_MAX,
-                op0=ALU.max,
-                op1=ALU.min,
-            )
+            if jj == HALF - 1:
+                pr["o"] = o
+                return
+            clamp(o[:, jj, :], pr["s"][j][:])
             last = g == n_groups - 1 and hh == GROUP // HALF - 1
             if last and jj == 1:
                 nc.sync.dma_start(out=out_v[g, hh][:, 0:2, :], in_=o[:, 0:2, :])
-            elif last and jj >= 2:
-                nc.sync.dma_start(out=out_v[g, hh][:, jj : jj + 1, :], in_=o[:, jj : jj + 1, :])
-            elif jj == HALF - 1:
-                nc.sync.dma_start(out=out_v[g, hh], in_=o[:])
+            elif last and jj == 2:
+                nc.sync.dma_start(out=out_v[g, hh][:, 2:3, :], in_=o[:, 2:3, :])
+
+        def op_m_copy(pr):
+            if "o" in pr:
+                raw_s = stage.tile([P, NI], F32, name="raw_s")
+                nc.scalar.copy(out=raw_s[:], in_=pr["s"][1][:])
+                pr["raw_s"] = raw_s
+
+        def op_m_clamp(pr):
+            if "o" in pr:
+                g = pr["g"]
+                hh = pr["j0"] // HALF
+                clamp(pr["o"][:, HALF - 1, :], pr["raw_s"][:])
+                if g == n_groups - 1 and hh == GROUP // HALF - 1:
+                    nc.sync.dma_start(out=out_v[g, hh][:, 3:4, :], in_=pr["o"][:, 3:4, :])
+                else:
+                    nc.sync.dma_start(out=out_v[g, hh], in_=pr["o"][:])
 
         def at(i, fn, *args):
             if 0 <= i < n_pairs:
                 fn(pairs[i], *args)
 
-        for n in range(-4, n_pairs + 6):
+        for n in range(-4, n_pairs + 7):
             at(n, op_e, 0)
             at(n, op_e, 1)
             op_q(n)
+            at(n - 7, op_m_clamp)
             at(n - 2, op_min)
             at(n - 6, op_m, 0)
             at(n - 6, op_m, 1)
@@ -305,5 +321,6 @@ def tile_net_pb_t_kernel(tc, h_user, h_item, uW2, ub2, iW2, ib2, out):
             at(n + 3, op_cp1, n)
             at(n - 1, op_rsqrt)
             at(n - 4, op_j, n)
+            at(n - 6, op_m_copy)
             if n == -3:
                 nc.scalar.copy(out=wg_i[:, W_SPLIT:D, :], in_=raw_i[:, :, W_SPLIT:D].rearrange("p t c -> p c t"))

@@ -34,10 +34,10 @@ def tile_net_pb_t_kernel(tc, h_user, h_item, uW2, ub2, iW2, ib2, out):
         vpool = ctx.enter_context(tc.tile_pool(name="vpool", bufs=10))
         small = ctx.enter_context(tc.tile_pool(name="small", bufs=6))
         opool = ctx.enter_context(tc.tile_pool(name="opool", bufs=4))
-        ps_h = ctx.enter_context(tc.psum_pool(name="ps_h", bufs=2))
-        ps_u = ctx.enter_context(tc.psum_pool(name="ps_u", bufs=2))
-        ps_t = ctx.enter_context(tc.psum_pool(name="ps_t", bufs=2))
-        ps_s = ctx.enter_context(tc.psum_pool(name="ps_s", bufs=2))
+        ps_h = ctx.enter_context(tc.psum_pool(name="ps_h", bufs=1))
+        ps_u = ctx.enter_context(tc.psum_pool(name="ps_u", bufs=3))
+        ps_t = ctx.enter_context(tc.psum_pool(name="ps_t", bufs=1))
+        ps_s = ctx.enter_context(tc.psum_pool(name="ps_s", bufs=3))
         ctx.enter_context(tc.manual_schedule())
 
         brow = const.tile([P, 2, D], BF16, name="brow")
@@ -127,7 +127,7 @@ def tile_net_pb_t_kernel(tc, h_user, h_item, uW2, ub2, iW2, ib2, out):
         grouped = {}
 
         def op_group(n):
-            if 0 <= n + 3 < n_pairs or 0 <= n - 4 < n_pairs:
+            if 0 <= n + 2 < n_pairs or 0 <= n - 3 < n_pairs:
                 g_new = stage.tile([P, 4 * D], BF16, name="gt", align_bytes=64)
                 grouped[n] = g_new
 
@@ -138,12 +138,12 @@ def tile_net_pb_t_kernel(tc, h_user, h_item, uW2, ub2, iW2, ib2, out):
             )
 
         def op_q(n):
-            has_h = 0 <= n + 2 < n_pairs
-            has_u = 0 <= n - 5 < n_pairs
+            has_h = 0 <= n + 1 < n_pairs
+            has_u = 0 <= n - 4 < n_pairs
             if not has_h and not has_u:
                 return
             gt = grouped[n - 1]
-            item = pairs[n - 5]["item"] if has_u else None
+            item = pairs[n - 4]["item"] if has_u else None
             if item is not None:
                 cols = slice(item * 2 * P, (item + 1) * 2 * P)
                 nc.vector.quantize_mx(out=itc[:, cols].bitcast(FP8X4), scales=its[:, cols], in_=gt[:, 2 * D : 4 * D])
@@ -156,11 +156,11 @@ def tile_net_pb_t_kernel(tc, h_user, h_item, uW2, ub2, iW2, ib2, out):
                 out=qc[:, w0:w1].bitcast(FP8X4), scales=qs[:, w0:w1], in_=gt[:, 4 * w0 : 4 * w1]
             )
             if has_h:
-                pairs[n + 2]["hc"] = qc
-                pairs[n + 2]["hs"] = qs
+                pairs[n + 1]["hc"] = qc
+                pairs[n + 1]["hs"] = qs
             if has_u:
-                pairs[n - 5]["uc"] = qc
-                pairs[n - 5]["us"] = qs
+                pairs[n - 4]["uc"] = qc
+                pairs[n - 4]["us"] = qs
 
         def op_a(pr, j):
             cols = slice(j * P, (j + 1) * P)
@@ -285,22 +285,21 @@ def tile_net_pb_t_kernel(tc, h_user, h_item, uW2, ub2, iW2, ib2, out):
             if 0 <= i < n_pairs:
                 fn(pairs[i], *args)
 
-        for n in range(-4, n_pairs + 7):
+        for n in range(-3, n_pairs + 6):
+            op_q(n)
+            at(n - 5, op_m_clamp)
+            at(n - 2, op_min)
             at(n, op_e, 0)
             at(n, op_e, 1)
-            op_q(n)
-            at(n - 7, op_m_clamp)
-            at(n - 2, op_min)
-            at(n - 6, op_m, 0)
-            at(n - 6, op_m, 1)
-            if n == -2:
+            at(n - 4, op_c, 0)
+            at(n - 4, op_c, 1)
+            at(n - 4, op_m, 0)
+            at(n - 4, op_m, 1)
+            if n == -1:
                 nc.vector.quantize_mx(
                     out=wc_i[:].bitcast(FP8X4), scales=ws_i[:], in_=wg_i[:].rearrange("p c t -> p (c t)")
                 )
-                spread_biases()
-                nc.vector.tensor_copy(out=bias_i[:], in_=bias_ps[0][:])
-                nc.vector.tensor_copy(out=bias_u[:], in_=bias_ps[1][:])
-            if n == 1:
+            if n == 0:
                 nc.vector.quantize_mx(
                     out=wc_u[:].bitcast(FP8X4), scales=ws_u[:], in_=wg_u[:].rearrange("p c t -> p (c t)")
                 )
@@ -308,19 +307,19 @@ def tile_net_pb_t_kernel(tc, h_user, h_item, uW2, ub2, iW2, ib2, out):
             at(n - 2, op_h, 1)
             at(n + 1, op_a, 0)
             at(n + 1, op_a, 1)
-            at(n - 3, op_t2)
-            if n == -1:
-                at(2, op_t1)
-            if n != -2:
-                at(n + 4, op_t1)
-            at(n - 5, op_c, 0)
-            at(n - 5, op_c, 1)
+            if n == -2:
+                spread_biases()
             op_group(n)
-            at(n - 1, op_f, 0)
-            at(n - 1, op_f, 1)
-            at(n + 3, op_cp1, n)
+            at(n + 2, op_cp1, n)
             at(n - 1, op_rsqrt)
-            at(n - 4, op_j, n)
-            at(n - 6, op_m_copy)
-            if n == -3:
+            at(n - 3, op_j, n)
+            at(n - 4, op_m_copy)
+            at(n, op_f, 0)
+            at(n, op_f, 1)
+            if n == -2:
                 nc.scalar.copy(out=wg_i[:, W_SPLIT:D, :], in_=raw_i[:, :, W_SPLIT:D].rearrange("p t c -> p c t"))
+                nc.scalar.copy(out=bias_i[:], in_=bias_ps[0][:])
+            if n == -1:
+                nc.scalar.copy(out=bias_u[:], in_=bias_ps[1][:])
+            at(n + 3, op_t1)
+            at(n - 2, op_t2)

@@ -22,6 +22,9 @@ CLAMP_MIN = 1e-6
 CLAMP_MAX = 1.0
 
 FLOPS = 2 * NU * D * D + 2 * NI * D * D + 2 * NU * D * NI
+U_SCALAR = 160
+U_GPSIMD = 288
+LATE = 4
 W_SPLIT = 336
 
 
@@ -70,13 +73,13 @@ def tile_net_pb_t_kernel(tc, h_user, h_item, uW2, ub2, iW2, ib2, out):
         nc.sync.dma_start(out=brow[0:1, 0, :], in_=ib2.unsqueeze(0))
         nc.sync.dma_start(out=brow[0:1, 1, :], in_=ub2.unsqueeze(0))
         nc.sync.dma_start(out=xi[:, 2:4, :], in_=hi_v[:, 2:4, :])
+        load_weight(raw_u, uW2)
         xs = []
         for g in range(n_groups):
             xg = xpool.tile([P, GROUP, D], BF16, name="x%d" % g)
             src = h_user[g * rows : (g + 1) * rows, :].rearrange("(p j) k -> p j k", j=GROUP)
             if g == 0:
                 nc.sync.dma_start(out=xg[:, 0:HALF, :], in_=src[:, 0:HALF, :])
-                load_weight(raw_u, uW2)
                 nc.sync.dma_start(out=xg[:, HALF:GROUP, :], in_=src[:, HALF:GROUP, :])
             else:
                 nc.sync.dma_start(out=xg[:], in_=src)
@@ -95,9 +98,15 @@ def tile_net_pb_t_kernel(tc, h_user, h_item, uW2, ub2, iW2, ib2, out):
         wg_i = const.tile([P, D, 4], BF16, name="wg_i", align_bytes=64)
         nc.vector.tensor_copy(out=wg_i[:, 0:W_SPLIT, :], in_=raw_i[:, :, 0:W_SPLIT].rearrange("p t c -> p c t"))
         wg_u = const.tile([P, D, 4], BF16, name="wg_u", align_bytes=64)
-        nc.gpsimd.tensor_scalar(
-            out=wg_u[:], in0=raw_u[:].rearrange("p t c -> p c t"), scalar1=1.0, scalar2=0.0, op0=ALU.mult, op1=ALU.add
-        )
+        for c0 in range(U_GPSIMD, D, 112):
+            nc.gpsimd.tensor_scalar(
+                out=wg_u[:, c0 : c0 + 112, :],
+                in0=raw_u[:, :, c0 : c0 + 112].rearrange("p t c -> p c t"),
+                scalar1=1.0,
+                scalar2=0.0,
+                op0=ALU.mult,
+                op1=ALU.add,
+            )
         wc_i = const.tile([P, D], U32, name="wc_i", align_bytes=64)
         ws_i = const.tile([P, D], U8, name="ws_i", align_bytes=64)
         wc_u = const.tile([P, D], U32, name="wc_u", align_bytes=64)
@@ -127,9 +136,8 @@ def tile_net_pb_t_kernel(tc, h_user, h_item, uW2, ub2, iW2, ib2, out):
         grouped = {}
 
         def op_group(n):
-            if 0 <= n + 2 < n_pairs or 0 <= n - 3 < n_pairs:
-                g_new = stage.tile([P, 4 * D], BF16, name="gt", align_bytes=64)
-                grouped[n] = g_new
+            g_new = stage.tile([P, 4 * D], BF16, name="gt", align_bytes=64)
+            grouped[n] = g_new
 
         def op_cp1(pr, n):
             nc.scalar.copy(
@@ -139,12 +147,12 @@ def tile_net_pb_t_kernel(tc, h_user, h_item, uW2, ub2, iW2, ib2, out):
 
         def op_q(n):
             has_h = 0 <= n + 1 < n_pairs
-            has_u = 0 <= n - 4 < n_pairs
+            has_u = 0 <= n - 4
             if not has_h and not has_u:
                 return
             gt = grouped[n - 1]
-            item = pairs[n - 4]["item"] if has_u else None
-            if item is not None:
+            if has_u and pairs[n - 4]["item"] is not None:
+                item = pairs[n - 4]["item"]
                 cols = slice(item * 2 * P, (item + 1) * 2 * P)
                 nc.vector.quantize_mx(out=itc[:, cols].bitcast(FP8X4), scales=its[:, cols], in_=gt[:, 2 * D : 4 * D])
                 has_u = False
@@ -161,6 +169,15 @@ def tile_net_pb_t_kernel(tc, h_user, h_item, uW2, ub2, iW2, ib2, out):
             if has_u:
                 pairs[n - 4]["uc"] = qc
                 pairs[n - 4]["us"] = qs
+
+        def op_q_un(pr, n):
+            qc = stage.tile([P, 4 * P], U32, name="qc", align_bytes=64)
+            qs = stage.tile([P, 4 * P], U8, name="qs", align_bytes=64)
+            nc.vector.quantize_mx(
+                out=qc[:, 2 * P : 4 * P].bitcast(FP8X4), scales=qs[:, 2 * P : 4 * P], in_=grouped[n][:, 2 * D : 4 * D]
+            )
+            pr["uc"] = qc
+            pr["us"] = qs
 
         def op_a(pr, j):
             cols = slice(j * P, (j + 1) * P)
@@ -198,9 +215,9 @@ def tile_net_pb_t_kernel(tc, h_user, h_item, uW2, ub2, iW2, ib2, out):
             nc.vector.tensor_scalar_min(out=rn[:], in0=pr["rcp"][:], scalar1=1.0 / EPS_NORM)
             pr["rn"] = rn
 
-        def op_h(pr, j):
+        def op_h(pr, j, engine):
             un = vpool.tile([P, D], BF16, name="un")
-            nc.gpsimd.tensor_scalar(
+            engine.tensor_scalar(
                 out=un[:],
                 in0=pr["v"][j][:],
                 scalar1=pr["rn"][:, j : j + 1],
@@ -210,8 +227,8 @@ def tile_net_pb_t_kernel(tc, h_user, h_item, uW2, ub2, iW2, ib2, out):
             )
             pr["un"].append(un)
 
-        def op_t2(pr):
-            unT = ps_t.tile([P, 2, 2, P], F32, name="unT")
+        def op_t2(pr, pool, name):
+            unT = pool.tile([P, 2, 2, P], F32, name=name)
             for j in range(2):
                 uw = pr["un"][j][:].bitcast(F32)
                 for u in range(2):
@@ -224,11 +241,11 @@ def tile_net_pb_t_kernel(tc, h_user, h_item, uW2, ub2, iW2, ib2, out):
                 in_=pr["unT"][:].rearrange("p j u r -> p j r u"),
             )
 
-        def op_c(pr, j):
+        def op_c(pr, j, pool, name):
             if pr["item"] is not None:
                 return
             cols = slice((2 + j) * P, (3 + j) * P)
-            s_ps = ps_s.tile([P, NI], F32, name="s_ps")
+            s_ps = pool.tile([P, NI], F32, name=name)
             nc.tensor.matmul_mx(
                 out=s_ps[:],
                 lhsT=pr["uc"][:, cols].bitcast(FP8X4),
@@ -245,66 +262,81 @@ def tile_net_pb_t_kernel(tc, h_user, h_item, uW2, ub2, iW2, ib2, out):
                 out=dst, in0=src, scalar1=CLAMP_MIN, scalar2=CLAMP_MAX, op0=ALU.max, op1=ALU.min
             )
 
-        def op_m(pr, j):
-            if pr["item"] is not None:
-                return
+        def o_tile(pr):
+            key = (pr["g"], pr["j0"] // HALF)
+            if key not in o_tiles:
+                o_new = opool.tile([P, HALF, NI], F32, name="o")
+                o_tiles[key] = o_new
+            return o_tiles[key]
+
+        def store(pr, j):
             g = pr["g"]
             hh = pr["j0"] // HALF
             jj = pr["j0"] % HALF + j
-            if jj == 0:
-                o_new = opool.tile([P, HALF, NI], F32, name="o")
-                o_tiles[(g, hh)] = o_new
             o = o_tiles[(g, hh)]
-            if jj == HALF - 1:
-                pr["o"] = o
-                return
-            clamp(o[:, jj, :], pr["s"][j][:])
-            last = g == n_groups - 1 and hh == GROUP // HALF - 1
-            if last and jj == 1:
-                nc.sync.dma_start(out=out_v[g, hh][:, 0:2, :], in_=o[:, 0:2, :])
-            elif last and jj == 2:
-                nc.sync.dma_start(out=out_v[g, hh][:, 2:3, :], in_=o[:, 2:3, :])
+            if pr in pairs[-LATE:]:
+                lo = jj
+            elif pr in pairs[-LATE:]:
+                lo = jj - 1 if j == 1 else None
+            else:
+                lo = 0 if jj == HALF - 1 else None
+            if lo is not None:
+                nc.sync.dma_start(out=out_v[g, hh][:, lo : jj + 1, :], in_=o[:, lo : jj + 1, :])
 
-        def op_m_copy(pr):
-            if "o" in pr:
+        def shared(k):
+            return k % 2 == 1 or k >= n_pairs - LATE
+
+        def op_m(k):
+            pr = pairs[k]
+            if pr["item"] is not None:
+                return
+            jj = pr["j0"] % HALF
+            clamp(o_tile(pr)[:, jj, :], pr["s"][0][:])
+            store(pr, 0)
+            if not shared(k):
+                clamp(o_tile(pr)[:, jj + 1, :], pr["s"][1][:])
+                store(pr, 1)
+
+        def op_m_copy(k):
+            pr = pairs[k]
+            if pr["item"] is None and shared(k):
                 raw_s = stage.tile([P, NI], F32, name="raw_s")
                 nc.scalar.copy(out=raw_s[:], in_=pr["s"][1][:])
                 pr["raw_s"] = raw_s
 
-        def op_m_clamp(pr):
-            if "o" in pr:
-                g = pr["g"]
-                hh = pr["j0"] // HALF
-                clamp(pr["o"][:, HALF - 1, :], pr["raw_s"][:])
-                if g == n_groups - 1 and hh == GROUP // HALF - 1:
-                    nc.sync.dma_start(out=out_v[g, hh][:, 3:4, :], in_=pr["o"][:, 3:4, :])
-                else:
-                    nc.sync.dma_start(out=out_v[g, hh], in_=pr["o"][:])
+        def op_m_clamp(k):
+            pr = pairs[k]
+            if pr["item"] is None and shared(k):
+                jj = pr["j0"] % HALF + 1
+                clamp(o_tile(pr)[:, jj, :], pr["raw_s"][:])
+                store(pr, 1)
 
         def at(i, fn, *args):
             if 0 <= i < n_pairs:
                 fn(pairs[i], *args)
 
-        for n in range(-3, n_pairs + 6):
+        for n in range(-3, n_pairs):
             op_q(n)
-            at(n - 5, op_m_clamp)
+            if n >= 5:
+                op_m_clamp(n - 5)
             at(n - 2, op_min)
             at(n, op_e, 0)
             at(n, op_e, 1)
-            at(n - 4, op_c, 0)
-            at(n - 4, op_c, 1)
-            at(n - 4, op_m, 0)
-            at(n - 4, op_m, 1)
+            at(n - 4, op_c, 0, ps_s, "s_ps")
+            at(n - 4, op_c, 1, ps_s, "s_ps")
+            if n >= 4:
+                op_m(n - 4)
             if n == -1:
                 nc.vector.quantize_mx(
                     out=wc_i[:].bitcast(FP8X4), scales=ws_i[:], in_=wg_i[:].rearrange("p c t -> p (c t)")
                 )
+                nc.vector.tensor_copy(out=wg_u[:, 0:U_SCALAR, :], in_=raw_u[:, :, 0:U_SCALAR].rearrange("p t c -> p c t"))
             if n == 0:
                 nc.vector.quantize_mx(
                     out=wc_u[:].bitcast(FP8X4), scales=ws_u[:], in_=wg_u[:].rearrange("p c t -> p (c t)")
                 )
-            at(n - 2, op_h, 0)
-            at(n - 2, op_h, 1)
+            at(n - 2, op_h, 0, nc.gpsimd)
+            at(n - 2, op_h, 1, nc.gpsimd)
             at(n + 1, op_a, 0)
             at(n + 1, op_a, 1)
             if n == -2:
@@ -313,7 +345,8 @@ def tile_net_pb_t_kernel(tc, h_user, h_item, uW2, ub2, iW2, ib2, out):
             at(n + 2, op_cp1, n)
             at(n - 1, op_rsqrt)
             at(n - 3, op_j, n)
-            at(n - 4, op_m_copy)
+            if n >= 4:
+                op_m_copy(n - 4)
             at(n, op_f, 0)
             at(n, op_f, 1)
             if n == -2:
@@ -321,5 +354,51 @@ def tile_net_pb_t_kernel(tc, h_user, h_item, uW2, ub2, iW2, ib2, out):
                 nc.scalar.copy(out=bias_i[:], in_=bias_ps[0][:])
             if n == -1:
                 nc.scalar.copy(out=bias_u[:], in_=bias_ps[1][:])
+                nc.scalar.copy(
+                    out=wg_u[:, U_SCALAR:U_GPSIMD, :], in_=raw_u[:, :, U_SCALAR:U_GPSIMD].rearrange("p t c -> p c t")
+                )
             at(n + 3, op_t1)
-            at(n - 2, op_t2)
+            at(n - 2, op_t2, ps_t, "unT")
+
+        ia, ib, ic, id_ = n_pairs - 4, n_pairs - 3, n_pairs - 2, n_pairs - 1
+        a, b, c, e = pairs[-4:]
+        op_q_un(a, n_pairs - 1)
+        op_m_clamp(ia - 1)
+        op_min(c)
+        op_h(c, 0, nc.vector)
+        op_h(c, 1, nc.vector)
+        op_c(a, 0, ps_s, "s_ps")
+        op_c(a, 1, ps_s, "s_ps")
+        op_rsqrt(e)
+        op_group(n_pairs)
+        op_j(b, n_pairs)
+        op_min(e)
+        op_h(e, 0, nc.vector)
+        op_h(e, 1, nc.vector)
+        op_t2(c, ps_h, "hT")
+        op_t2(e, ps_t, "unT")
+        op_group(n_pairs + 1)
+        op_j(c, n_pairs + 1)
+        op_m(ia)
+        op_m_copy(ia)
+        op_q_un(b, n_pairs)
+        op_q_un(c, n_pairs + 1)
+        op_c(b, 0, ps_s, "s_ps")
+        op_c(b, 1, ps_u, "u_ps")
+        op_c(c, 0, ps_u, "u_ps")
+        op_c(c, 1, ps_u, "u_ps")
+        op_group(n_pairs + 2)
+        op_j(e, n_pairs + 2)
+        op_m_clamp(ia)
+        op_m(ib)
+        op_q_un(e, n_pairs + 2)
+        op_m_copy(ib)
+        op_m_copy(ic)
+        op_c(e, 0, ps_s, "s_ps")
+        op_c(e, 1, ps_s, "s_ps")
+        op_m(ic)
+        op_m_clamp(ib)
+        op_m_clamp(ic)
+        op_m_copy(id_)
+        op_m(id_)
+        op_m_clamp(id_)

@@ -43,6 +43,11 @@ def tile_net_pb_t_kernel(tc, h_user, h_item, uW2, ub2, iW2, ib2, out):
         ps_s = ctx.enter_context(tc.psum_pool(name="ps_s", bufs=3))
         ctx.enter_context(tc.manual_schedule())
 
+        wz = const.tile([P, D], BF16, name="wz")
+        nc.vector.memset(wz[:], 1.0)
+        for i in range(5):
+            w_ps = ps_s.tile([P, D], F32, name="s_ps")
+            nc.tensor.matmul(out=w_ps[:], lhsT=wz[:, 0:P], rhs=wz[:], start=True, stop=True)
         brow = const.tile([P, 2, D], BF16, name="brow")
         nc.vector.memset(brow[:], 0.0)
         ones = const.tile([P, P], BF16, name="ones")
@@ -284,7 +289,7 @@ def tile_net_pb_t_kernel(tc, h_user, h_item, uW2, ub2, iW2, ib2, out):
                 nc.sync.dma_start(out=out_v[g, hh][:, lo : jj + 1, :], in_=o[:, lo : jj + 1, :])
 
         def shared(k):
-            return k % 2 == 1 or k >= n_pairs - LATE
+            return k % 3 != 0 or k >= n_pairs - LATE
 
         def op_m(k):
             pr = pairs[k]

@@ -24,6 +24,7 @@ CLAMP_MAX = 1.0
 FLOPS = 2 * NU * D * D + 2 * NI * D * D + 2 * NU * D * NI
 U_SCALAR = 160
 U_GPSIMD = 288
+SHARE = 160
 LATE = 4
 W_SPLIT = 336
 
@@ -288,8 +289,8 @@ def tile_net_pb_t_kernel(tc, h_user, h_item, uW2, ub2, iW2, ib2, out):
             if lo is not None:
                 nc.sync.dma_start(out=out_v[g, hh][:, lo : jj + 1, :], in_=o[:, lo : jj + 1, :])
 
-        def shared(k):
-            return k % 3 != 0 or k >= n_pairs - LATE
+        def first_shared(k):
+            return 0 if k >= n_pairs - LATE else SHARE
 
         def op_m(k):
             pr = pairs[k]
@@ -298,22 +299,24 @@ def tile_net_pb_t_kernel(tc, h_user, h_item, uW2, ub2, iW2, ib2, out):
             jj = pr["j0"] % HALF
             clamp(o_tile(pr)[:, jj, :], pr["s"][0][:])
             store(pr, 0)
-            if not shared(k):
-                clamp(o_tile(pr)[:, jj + 1, :], pr["s"][1][:])
-                store(pr, 1)
+            c0 = first_shared(k)
+            if c0 > 0:
+                clamp(o_tile(pr)[:, jj + 1, 0:c0], pr["s"][1][:, 0:c0])
 
         def op_m_copy(k):
             pr = pairs[k]
-            if pr["item"] is None and shared(k):
+            if pr["item"] is None:
+                c0 = first_shared(k)
                 raw_s = stage.tile([P, NI], F32, name="raw_s")
-                nc.scalar.copy(out=raw_s[:], in_=pr["s"][1][:])
+                nc.scalar.copy(out=raw_s[:, c0:NI], in_=pr["s"][1][:, c0:NI])
                 pr["raw_s"] = raw_s
 
         def op_m_clamp(k):
             pr = pairs[k]
-            if pr["item"] is None and shared(k):
+            if pr["item"] is None:
                 jj = pr["j0"] % HALF + 1
-                clamp(o_tile(pr)[:, jj, :], pr["raw_s"][:])
+                c0 = first_shared(k)
+                clamp(o_tile(pr)[:, jj, c0:NI], pr["raw_s"][:, c0:NI])
                 store(pr, 1)
 
         def at(i, fn, *args):
@@ -322,13 +325,19 @@ def tile_net_pb_t_kernel(tc, h_user, h_item, uW2, ub2, iW2, ib2, out):
 
         for n in range(-3, n_pairs):
             op_q(n)
+            at(n - 2, op_min)
             if n >= 5:
                 op_m_clamp(n - 5)
-            at(n - 2, op_min)
             at(n, op_e, 0)
             at(n, op_e, 1)
             at(n - 4, op_c, 0, ps_s, "s_ps")
             at(n - 4, op_c, 1, ps_s, "s_ps")
+            op_group(n)
+            at(n + 2, op_cp1, n)
+            at(n - 1, op_rsqrt)
+            at(n - 3, op_j, n)
+            if n >= 4:
+                op_m_copy(n - 4)
             if n >= 4:
                 op_m(n - 4)
             if n == -1:
@@ -346,12 +355,6 @@ def tile_net_pb_t_kernel(tc, h_user, h_item, uW2, ub2, iW2, ib2, out):
             at(n + 1, op_a, 1)
             if n == -2:
                 spread_biases()
-            op_group(n)
-            at(n + 2, op_cp1, n)
-            at(n - 1, op_rsqrt)
-            at(n - 3, op_j, n)
-            if n >= 4:
-                op_m_copy(n - 4)
             at(n, op_f, 0)
             at(n, op_f, 1)
             if n == -2:

@@ -125,10 +125,10 @@ def tile_net_pb_t_kernel(tc, h_user, h_item, uW2, ub2, iW2, ib2, out):
 
         pairs = []
         for k in range(NI // (2 * P)):
-            pairs.append({"x": xi, "j0": 2 * k, "wc": wc_i, "ws": ws_i, "bias": bias_i, "item": k, "v": [], "un": [], "u": [], "s": []})
+            pairs.append({"x": xi, "j0": 2 * k, "wc": wc_i, "ws": ws_i, "bias": bias_i, "item": k, "v": [], "un": {}, "u": [], "s": []})
         for g in range(n_groups):
             for k in range(GROUP // 2):
-                pairs.append({"x": xs[g], "j0": 2 * k, "wc": wc_u, "ws": ws_u, "bias": bias_u, "item": None, "g": g, "v": [], "un": [], "u": [], "s": []})
+                pairs.append({"x": xs[g], "j0": 2 * k, "wc": wc_u, "ws": ws_u, "bias": bias_u, "item": None, "g": g, "v": [], "un": {}, "u": [], "s": []})
         n_pairs = len(pairs)
         o_tiles = {}
         def op_t1(pr):
@@ -223,6 +223,7 @@ def tile_net_pb_t_kernel(tc, h_user, h_item, uW2, ub2, iW2, ib2, out):
 
         def op_h(pr, j, engine):
             un = vpool.tile([P, D], BF16, name="un")
+            pr["un"][j] = un
             engine.tensor_scalar(
                 out=un[:],
                 in0=pr["v"][j][:],
@@ -231,7 +232,6 @@ def tile_net_pb_t_kernel(tc, h_user, h_item, uW2, ub2, iW2, ib2, out):
                 op0=ALU.mult,
                 op1=ALU.add,
             )
-            pr["un"].append(un)
 
         def op_t2(pr, pool, name):
             unT = pool.tile([P, 2, 2, P], F32, name=name)
@@ -330,6 +330,8 @@ def tile_net_pb_t_kernel(tc, h_user, h_item, uW2, ub2, iW2, ib2, out):
                 op_m_clamp(n - 5)
             at(n, op_e, 0)
             at(n, op_e, 1)
+            if n - 2 < 4:
+                at(n - 2, op_h, 1, nc.vector)
             at(n - 4, op_c, 0, ps_s, "s_ps")
             at(n - 4, op_c, 1, ps_s, "s_ps")
             op_group(n)
@@ -350,7 +352,8 @@ def tile_net_pb_t_kernel(tc, h_user, h_item, uW2, ub2, iW2, ib2, out):
                     out=wc_u[:].bitcast(FP8X4), scales=ws_u[:], in_=wg_u[:].rearrange("p c t -> p (c t)")
                 )
             at(n - 2, op_h, 0, nc.gpsimd)
-            at(n - 2, op_h, 1, nc.gpsimd)
+            if n - 2 >= 4:
+                at(n - 2, op_h, 1, nc.gpsimd)
             at(n + 1, op_a, 0)
             at(n + 1, op_a, 1)
             if n == -2:

from contextlib import ExitStack

import concourse.mybir as mybir
from concourse.masks import make_identity

F32 = mybir.dt.float32
BF16 = mybir.dt.bfloat16
U32 = mybir.dt.uint32
U8 = mybir.dt.uint8
FP8X4 = mybir.dt.float8_e4m3fn_x4
ALU = mybir.AluOpType
ACTF = mybir.ActivationFunctionType

P = 128
D = 512
NU = 8192
NI = 512
GROUP = 8
HALF = 4
EPS_NORM = 1e-8
CLAMP_MIN = 1e-6
CLAMP_MAX = 1.0

FLOPS = 2 * NU * D * D + 2 * NI * D * D + 2 * NU * D * NI
U_SCALAR = 160
U_GPSIMD = 288
SHARE = 160
LATE = 4
W_SPLIT = 336


def tile_net_pb_t_kernel(tc, h_user, h_item, uW2, ub2, iW2, ib2, out):
    nc = tc.nc
    with ExitStack() as ctx:
        const = ctx.enter_context(tc.tile_pool(name="const", bufs=1))
        xpool = ctx.enter_context(tc.tile_pool(name="xpool", bufs=1))
        stage = ctx.enter_context(tc.tile_pool(name="stage", bufs=3))
        vpool = ctx.enter_context(tc.tile_pool(name="vpool", bufs=10))
        small = ctx.enter_context(tc.tile_pool(name="small", bufs=6))
        opool = ctx.enter_context(tc.tile_pool(name="opool", bufs=4))
        ps_h = ctx.enter_context(tc.psum_pool(name="ps_h", bufs=1))
        ps_u = ctx.enter_context(tc.psum_pool(name="ps_u", bufs=3))
        ps_t = ctx.enter_context(tc.psum_pool(name="ps_t", bufs=1))
        ps_s = ctx.enter_context(tc.psum_pool(name="ps_s", bufs=3))
        ctx.enter_context(tc.manual_schedule())

        wz = const.tile([P, D], BF16, name="wz")
        nc.vector.memset(wz[:], 1.0)
        for i in range(5):
            w_ps = ps_s.tile([P, D], F32, name="s_ps")
            nc.tensor.matmul(out=w_ps[:], lhsT=wz[:, 0:P], rhs=wz[:], start=True, stop=True)
        brow = const.tile([P, 2, D], BF16, name="brow")
        nc.vector.memset(brow[:], 0.0)
        ones = const.tile([P, P], BF16, name="ones")
        nc.vector.memset(ones[:], 1.0)
        one = const.tile([P, 1], F32, name="one")
        nc.vector.memset(one[:], 1.0)
        ident_f = const.tile([P, P], F32, name="ident_f")
        make_identity(nc, ident_f[:])

        warm = const.tile([P, 1], F32, name="warm")
        nc.scalar.activation(out=warm[:], in_=one[:], func=ACTF.Abs_reciprocal_sqrt)

        n_groups = NU // (P * GROUP)
        rows = P * GROUP
        xi = xpool.tile([P, NI // P, D], BF16, name="xi")
        hi_v = h_item.rearrange("(j p) k -> p j k", p=P)
        raw_i = const.tile([P, 4, D], BF16, name="raw_i")
        raw_u = const.tile([P, 4, D], BF16, name="raw_u")

        def load_weight(raw, w):
            nc.sync.dma_start(
                out=raw[:].rearrange("q (u e) c -> q u e c", u=2),
                in_=w.rearrange("(u q e) c -> q u e c", u=2, e=2),
            )

        nc.sync.dma_start(out=xi[:, 0:2, :], in_=hi_v[:, 0:2, :])
        load_weight(raw_i, iW2)
        nc.sync.dma_start(out=brow[0:1, 0, :], in_=ib2.unsqueeze(0))
        nc.sync.dma_start(out=brow[0:1, 1, :], in_=ub2.unsqueeze(0))
        nc.sync.dma_start(out=xi[:, 2:4, :], in_=hi_v[:, 2:4, :])
        load_weight(raw_u, uW2)
        xs = []
        for g in range(n_groups):
            xg = xpool.tile([P, GROUP, D], BF16, name="x%d" % g)
            src = h_user[g * rows : (g + 1) * rows, :].rearrange("(p j) k -> p j k", j=GROUP)
            if g == 0:
                nc.sync.dma_start(out=xg[:, 0:HALF, :], in_=src[:, 0:HALF, :])
                nc.sync.dma_start(out=xg[:, HALF:GROUP, :], in_=src[:, HALF:GROUP, :])
            else:
                nc.sync.dma_start(out=xg[:], in_=src)
            xs.append(xg)

        bias_i = const.tile([P, D], F32, name="bias_i")
        bias_u = const.tile([P, D], F32, name="bias_u")
        bias_ps = []

        def spread_biases():
            for k in range(2):
                b_ps = ps_u.tile([P, D], F32, name="u_ps")
                nc.tensor.matmul(out=b_ps[:], lhsT=ones[:], rhs=brow[:, k, :], start=True, stop=True)
                bias_ps.append(b_ps)

        wg_i = const.tile([P, D, 4], BF16, name="wg_i", align_bytes=64)
        nc.vector.tensor_copy(out=wg_i[:, 0:W_SPLIT, :], in_=raw_i[:, :, 0:W_SPLIT].rearrange("p t c -> p c t"))
        wg_u = const.tile([P, D, 4], BF16, name="wg_u", align_bytes=64)
        for c0 in range(U_GPSIMD, D, 112):
            nc.gpsimd.tensor_scalar(
                out=wg_u[:, c0 : c0 + 112, :],
                in0=raw_u[:, :, c0 : c0 + 112].rearrange("p t c -> p c t"),
                scalar1=1.0,
                scalar2=0.0,
                op0=ALU.mult,
                op1=ALU.add,
            )
        wc_i = const.tile([P, D], U32, name="wc_i", align_bytes=64)
        ws_i = const.tile([P, D], U8, name="ws_i", align_bytes=64)
        wc_u = const.tile([P, D], U32, name="wc_u", align_bytes=64)
        ws_u = const.tile([P, D], U8, name="ws_u", align_bytes=64)

        itc = const.tile([P, NI], U32, name="itc", align_bytes=64)
        its = const.tile([P, NI], U8, name="its", align_bytes=64)

        out_v = out.rearrange("(g p h j) n -> g h p j n", p=P, h=GROUP // HALF, j=HALF)

        pairs = []
        for k in range(NI // (2 * P)):
            pairs.append({"x": xi, "j0": 2 * k, "wc": wc_i, "ws": ws_i, "bias": bias_i, "item": k, "v": [], "un": {}, "u": [], "s": []})
        for g in range(n_groups):
            for k in range(GROUP // 2):
                pairs.append({"x": xs[g], "j0": 2 * k, "wc": wc_u, "ws": ws_u, "bias": bias_u, "item": None, "g": g, "v": [], "un": {}, "u": [], "s": []})
        n_pairs = len(pairs)
        o_tiles = {}
        def op_t1(pr):
            hT = ps_h.tile([P, 2, 2, P], F32, name="hT")
            for j in range(2):
                xw = pr["x"][:, pr["j0"] + j, :].bitcast(F32)
                for u in range(2):
                    nc.tensor.transpose(hT[:, j, u, :], xw[:, u * P : (u + 1) * P], ident_f[:])
            pr["hT"] = hT

        grouped = {}

        def op_group(n):
            g_new = stage.tile([P, 4 * D], BF16, name="gt", align_bytes=64)
            grouped[n] = g_new

        def op_cp1(pr, n):
            nc.scalar.copy(
                out=grouped[n][:, 0 : 2 * D].bitcast(F32).rearrange("p (j r u) -> p j r u", j=2, u=2),
                in_=pr["hT"][:].rearrange("p j u r -> p j r u"),
            )

        def op_q(n):
            has_h = 0 <= n + 1 < n_pairs
            has_u = 0 <= n - 4
            if not has_h and not has_u:
                return
            gt = grouped[n - 1]
            if has_u and pairs[n - 4]["item"] is not None:
                item = pairs[n - 4]["item"]
                cols = slice(item * 2 * P, (item + 1) * 2 * P)
                nc.vector.quantize_mx(out=itc[:, cols].bitcast(FP8X4), scales=its[:, cols], in_=gt[:, 2 * D : 4 * D])
                has_u = False
            qc = stage.tile([P, 4 * P], U32, name="qc", align_bytes=64)
            qs = stage.tile([P, 4 * P], U8, name="qs", align_bytes=64)
            w0 = 0 if has_h else 2 * P
            w1 = 4 * P if has_u else 2 * P
            nc.vector.quantize_mx(
                out=qc[:, w0:w1].bitcast(FP8X4), scales=qs[:, w0:w1], in_=gt[:, 4 * w0 : 4 * w1]
            )
            if has_h:
                pairs[n + 1]["hc"] = qc
                pairs[n + 1]["hs"] = qs
            if has_u:
                pairs[n - 4]["uc"] = qc
                pairs[n - 4]["us"] = qs

        def op_q_un(pr, n):
            qc = stage.tile([P, 4 * P], U32, name="qc", align_bytes=64)
            qs = stage.tile([P, 4 * P], U8, name="qs", align_bytes=64)
            nc.vector.quantize_mx(
                out=qc[:, 2 * P : 4 * P].bitcast(FP8X4), scales=qs[:, 2 * P : 4 * P], in_=grouped[n][:, 2 * D : 4 * D]
            )
            pr["uc"] = qc
            pr["us"] = qs

        def op_a(pr, j):
            cols = slice(j * P, (j + 1) * P)
            u_ps = ps_u.tile([P, D], F32, name="u_ps")
            nc.tensor.matmul_mx(
                out=u_ps[:],
                lhsT=pr["hc"][:, cols].bitcast(FP8X4),
                lhsT_scale=pr["hs"][:, cols],
                rhs=pr["wc"][:].bitcast(FP8X4),
                rhs_scale=pr["ws"][:],
                start=True,
                stop=True,
            )
            pr["u"].append(u_ps)

        def op_e(pr, j):
            v = vpool.tile([P, D], F32, name="v")
            nc.vector.tensor_tensor(out=v[:], in0=pr["u"][j][:], in1=pr["bias"][:], op=ALU.add)
            pr["v"].append(v)

        def op_f(pr, j):
            if j == 0:
                ss = small.tile([P, 2], F32, name="ss")
                pr["ss"] = ss
            junk = stage.tile([P, D], BF16, name="junk")
            nc.scalar.activation(out=junk[:], in_=pr["v"][j][:], func=ACTF.Square, accum_out=pr["ss"][:, j : j + 1])

        def op_rsqrt(pr):
            rcp = small.tile([P, 2], F32, name="rcp")
            nc.scalar.activation(out=rcp[:], in_=pr["ss"][:], func=ACTF.Abs_reciprocal_sqrt)
            pr["rcp"] = rcp

        def op_min(pr):
            rn = small.tile([P, 2], F32, name="rn")
            nc.vector.tensor_scalar_min(out=rn[:], in0=pr["rcp"][:], scalar1=1.0 / EPS_NORM)
            pr["rn"] = rn

        def op_h(pr, j, engine):
            un = vpool.tile([P, D], BF16, name="un")
            pr["un"][j] = un
            engine.tensor_scalar(
                out=un[:],
                in0=pr["v"][j][:],
                scalar1=pr["rn"][:, j : j + 1],
                scalar2=0.0,
                op0=ALU.mult,
                op1=ALU.add,
            )

        def op_t2(pr, pool, name):
            unT = pool.tile([P, 2, 2, P], F32, name=name)
            for j in range(2):
                uw = pr["un"][j][:].bitcast(F32)
                for u in range(2):
                    nc.tensor.transpose(unT[:, j, u, :], uw[:, u * P : (u + 1) * P], ident_f[:])
            pr["unT"] = unT

        def op_j(pr, n):
            nc.scalar.copy(
                out=grouped[n][:, 2 * D : 4 * D].bitcast(F32).rearrange("p (j r u) -> p j r u", j=2, u=2),
                in_=pr["unT"][:].rearrange("p j u r -> p j r u"),
            )

        def op_c(pr, j, pool, name):
            if pr["item"] is not None:
                return
            cols = slice((2 + j) * P, (3 + j) * P)
            s_ps = pool.tile([P, NI], F32, name=name)
            nc.tensor.matmul_mx(
                out=s_ps[:],
                lhsT=pr["uc"][:, cols].bitcast(FP8X4),
                lhsT_scale=pr["us"][:, cols],
                rhs=itc[:].bitcast(FP8X4),
                rhs_scale=its[:],
                start=True,
                stop=True,
            )
            pr["s"].append(s_ps)

        def clamp(dst, src):
            nc.vector.tensor_scalar(
                out=dst, in0=src, scalar1=CLAMP_MIN, scalar2=CLAMP_MAX, op0=ALU.max, op1=ALU.min
            )

        def o_tile(pr):
            key = (pr["g"], pr["j0"] // HALF)
            if key not in o_tiles:
                o_new = opool.tile([P, HALF, NI], F32, name="o")
                o_tiles[key] = o_new
            return o_tiles[key]

        def store(pr, j):
            g = pr["g"]
            hh = pr["j0"] // HALF
            jj = pr["j0"] % HALF + j
            o = o_tiles[(g, hh)]
            if pr in pairs[-LATE:]:
                lo = jj
            elif pr in pairs[-LATE:]:
                lo = jj - 1 if j == 1 else None
            else:
                lo = 0 if jj == HALF - 1 else None
            if lo is not None:
                nc.sync.dma_start(out=out_v[g, hh][:, lo : jj + 1, :], in_=o[:, lo : jj + 1, :])

        def first_shared(k):
            return 0 if k >= n_pairs - LATE else SHARE

        def op_m(k):
            pr = pairs[k]
            if pr["item"] is not None:
                return
            jj = pr["j0"] % HALF
            clamp(o_tile(pr)[:, jj, :], pr["s"][0][:])
            store(pr, 0)
            c0 = first_shared(k)
            if c0 > 0:
                clamp(o_tile(pr)[:, jj + 1, 0:c0], pr["s"][1][:, 0:c0])

        def op_m_copy(k):
            pr = pairs[k]
            if pr["item"] is None:
                c0 = first_shared(k)
                raw_s = stage.tile([P, NI], F32, name="raw_s")
                nc.scalar.copy(out=raw_s[:, c0:NI], in_=pr["s"][1][:, c0:NI])
                pr["raw_s"] = raw_s

        def op_m_clamp(k):
            pr = pairs[k]
            if pr["item"] is None:
                jj = pr["j0"] % HALF + 1
                c0 = first_shared(k)
                clamp(o_tile(pr)[:, jj, c0:NI], pr["raw_s"][:, c0:NI])
                store(pr, 1)

        def at(i, fn, *args):
            if 0 <= i < n_pairs:
                fn(pairs[i], *args)

        for n in range(-3, n_pairs):
            op_q(n)
            at(n - 2, op_min)
            if n >= 5:
                op_m_clamp(n - 5)
            at(n, op_e, 0)
            at(n, op_e, 1)
            if n - 2 < 4:
                at(n - 2, op_h, 1, nc.vector)
            at(n - 4, op_c, 0, ps_s, "s_ps")
            at(n - 4, op_c, 1, ps_s, "s_ps")
            op_group(n)
            at(n + 2, op_cp1, n)
            at(n - 1, op_rsqrt)
            at(n - 3, op_j, n)
            if n >= 4:
                op_m_copy(n - 4)
            if n >= 4:
                op_m(n - 4)
            if n == -1:
                nc.vector.quantize_mx(
                    out=wc_i[:].bitcast(FP8X4), scales=ws_i[:], in_=wg_i[:].rearrange("p c t -> p (c t)")
                )
                nc.vector.tensor_copy(out=wg_u[:, 0:U_SCALAR, :], in_=raw_u[:, :, 0:U_SCALAR].rearrange("p t c -> p c t"))
            if n == 0:
                nc.vector.quantize_mx(
                    out=wc_u[:].bitcast(FP8X4), scales=ws_u[:], in_=wg_u[:].rearrange("p c t -> p (c t)")
                )
            at(n - 2, op_h, 0, nc.gpsimd)
            if n - 2 >= 4:
                at(n - 2, op_h, 1, nc.gpsimd)
            at(n + 1, op_a, 0)
            at(n + 1, op_a, 1)
            if n == -2:
                spread_biases()
            at(n, op_f, 0)
            at(n, op_f, 1)
            if n == -2:
                nc.scalar.copy(out=wg_i[:, W_SPLIT:D, :], in_=raw_i[:, :, W_SPLIT:D].rearrange("p t c -> p c t"))
                nc.scalar.copy(out=bias_i[:], in_=bias_ps[0][:])
            if n == -1:
                nc.scalar.copy(out=bias_u[:], in_=bias_ps[1][:])
                nc.scalar.copy(
                    out=wg_u[:, U_SCALAR:U_GPSIMD, :], in_=raw_u[:, :, U_SCALAR:U_GPSIMD].rearrange("p t c -> p c t")
                )
            at(n + 3, op_t1)
            at(n - 2, op_t2, ps_t, "unT")

        ia, ib, ic, id_ = n_pairs - 4, n_pairs - 3, n_pairs - 2, n_pairs - 1
        a, b, c, e = pairs[-4:]
        op_q_un(a, n_pairs - 1)
        op_m_clamp(ia - 1)
        op_min(c)
        op_h(c, 0, nc.vector)
        op_h(c, 1, nc.vector)
        op_c(a, 0, ps_s, "s_ps")
        op_c(a, 1, ps_s, "s_ps")
        op_rsqrt(e)
        op_group(n_pairs)
        op_j(b, n_pairs)
        op_min(e)
        op_h(e, 0, nc.vector)
        op_h(e, 1, nc.vector)
        op_t2(c, ps_h, "hT")
        op_t2(e, ps_t, "unT")
        op_group(n_pairs + 1)
        op_j(c, n_pairs + 1)
        op_m(ia)
        op_m_copy(ia)
        op_q_un(b, n_pairs)
        op_q_un(c, n_pairs + 1)
        op_c(b, 0, ps_s, "s_ps")
        op_c(b, 1, ps_u, "u_ps")
        op_c(c, 0, ps_u, "u_ps")
        op_c(c, 1, ps_u, "u_ps")
        op_group(n_pairs + 2)
        op_j(e, n_pairs + 2)
        op_m_clamp(ia)
        op_m(ib)
        op_q_un(e, n_pairs + 2)
        op_m_copy(ib)
        op_m_copy(ic)
        op_c(e, 0, ps_s, "s_ps")
        op_c(e, 1, ps_s, "s_ps")
        op_m(ic)
        op_m_clamp(ib)
        op_m_clamp(ic)
        op_m_copy(id_)
        op_m(id_)
        op_m_clamp(id_)
